import numpy as np
import ml_dtypes


def mxq(x, axis, fmt="e4m3"):
    dtype, down = {"e4m3": (ml_dtypes.float8_e4m3fn, 7), "e5m2": (ml_dtypes.float8_e5m2, 14)}[fmt]
    v = np.moveaxis(np.asarray(x, np.float32).astype(ml_dtypes.bfloat16).astype(np.float64), axis, -1)
    blocks = v.reshape(v.shape[:-1] + (-1, 32))
    amax = np.abs(blocks).max(-1, keepdims=True)
    byte = np.maximum(np.where(amax > 0, np.frexp(amax)[1] - 1 + 127, 0) - down, 1)
    scale = np.exp2(byte - 127.0)
    codes = (blocks / scale).astype(np.float32).astype(dtype).astype(np.float64)
    return np.moveaxis((codes * scale).reshape(v.shape), -1, axis)


WIDE = False


def mx_kscale(k):
    if not WIDE:
        return np.ones(k)
    levels = np.array([10, -10, 5, -5, 0])
    a = np.random.permutation(np.resize(levels, k // 512 * 4)).reshape(k // 512, 4)
    idx = np.arange(k)
    return np.exp2(a[idx // 512, idx % 128 // 32])


BF16 = ml_dtypes.bfloat16


def bf(x):
    return np.asarray(x, np.float32).astype(BF16)


def f64(x):
    return np.asarray(x).astype(np.float64)


E, T, H, D, R = 2, 128, 512, 512, 128
SCALE = 2.0


def silu(v):
    return v / (1.0 + np.exp(-v))


def setup_inputs():
    s = mx_kscale(H)
    return {"x": bf(np.random.standard_normal((E, T, H)) * s),
            "low_gu": bf(np.random.standard_normal((E, T, R))),
            "W_gu": bf(np.random.standard_normal((E, 2 * D, H)) / np.sqrt(H) / s),
            "B_gu": bf(np.random.standard_normal((E, 2 * D, R)) * 0.3 / np.sqrt(R)),
            "A_d": bf(np.random.standard_normal((E, R, D)) * 1.5 / np.sqrt(D))}


def reference(x, low_gu, W_gu, B_gu, A_d):
    base = mxq(f64(x), 2, "e4m3") @ mxq(f64(W_gu), 2, "e4m3").transpose(0, 2, 1)
    delta = f64(low_gu) @ f64(B_gu).transpose(0, 2, 1)
    gate_up = base + SCALE * delta
    gate, up = gate_up[..., :D], gate_up[..., D:]
    h = up * silu(gate)
    low_d = mxq(h, 2, "e4m3") @ mxq(f64(A_d), 2, "e4m3").transpose(0, 2, 1)
    return h, low_d

@@ -1,0 +1,232 @@
+from contextlib import ExitStack
+
+import concourse.mybir as mybir
+from concourse.masks import make_identity
+
+F32 = mybir.dt.float32
+BF16 = mybir.dt.bfloat16
+U32 = mybir.dt.uint32
+U8 = mybir.dt.uint8
+FP8X4 = mybir.dt.float8_e4m3fn_x4
+ACT = mybir.ActivationFunctionType
+ALU = mybir.AluOpType
+
+E, T, H, D, R = 2, 128, 512, 512, 128
+LORA_SCALE = 2.0
+P = 128
+PACK = 4
+PAIR = 2
+HALVES = 2
+ROWS = D // P
+STEPS = 2
+J = ROWS // STEPS
+
+FLOPS = 2 * E * T * (H * 2 * D + R * 2 * D + D * R)
+
+
+def tile_loralinearexpertswrapper_pa_s_kernel(tc, x, low_gu, W_gu, B_gu, A_d, out_0, out_1):
+    nc = tc.nc
+    with ExitStack() as ctx:
+        keep = ctx.enter_context(tc.tile_pool(name="keep", bufs=1))
+        w_pool = ctx.enter_context(tc.tile_pool(name="w_pool", bufs=E * STEPS * HALVES))
+        work = ctx.enter_context(tc.tile_pool(name="work", bufs=3))
+        flip = ctx.enter_context(tc.psum_pool(name="flip", bufs=3))
+        sums = ctx.enter_context(tc.psum_pool(name="sums", bufs=4))
+        last = ctx.enter_context(tc.psum_pool(name="last", bufs=1))
+
+        low_sb = keep.tile([P, E, R], BF16)
+        nc.sync.dma_start(out=low_sb[:], in_=low_gu.rearrange("e t r -> t e r"))
+        b_sb = keep.tile([P, E, HALVES, ROWS * R], BF16)
+        b_rows = B_gu.rearrange("e (s p j) r -> e p s (j r)", s=HALVES, p=P)
+        for e in range(E):
+            nc.sync.dma_start(out=b_sb[:, e], in_=b_rows[e])
+        x_sb = keep.tile([P, E, H], BF16)
+        nc.sync.dma_start(out=x_sb[:], in_=x.rearrange("e t h -> t e h"))
+        pieces = [(e, a, s) for e in range(E) for a in range(STEPS) for s in range(HALVES)]
+        w_rows = W_gu.rearrange("e (s p a j) h -> e a s p (j h)", s=HALVES, p=P, a=STEPS)
+        w_raw = []
+        for e, a, s in pieces:
+            raw = w_pool.tile([P, J * H], BF16, name="w_raw")
+            nc.sync.dma_start(out=raw[:], in_=w_rows[e, a, s])
+            w_raw.append(raw)
+        a_sb = keep.tile([P, E, D], BF16)
+        nc.sync.dma_start(out=a_sb[:], in_=A_d.rearrange("e r d -> r e d"))
+
+        ident_f32 = keep.tile([P, P], F32)
+        make_identity(nc, ident_f32[:])
+        ident_bf16 = keep.tile([P, P], BF16)
+        make_identity(nc, ident_bf16[:])
+        zero = keep.tile([P, 1], F32)
+        nc.vector.memset(zero[:], 0.0)
+        unused = keep.tile([P, 1], F32)
+        nc.scalar.activation(out=unused[:], in_=zero[:], func=ACT.Silu)
+
+        low_t = flip.tile([P, E, T], BF16, tag="flip")
+        for e in range(E):
+            nc.tensor.transpose(low_t[:, e, :], low_sb[:, e, :], ident_bf16[:])
+        low_k = keep.tile([P, E, T], BF16)
+        nc.scalar.copy(out=low_k[:], in_=low_t[:])
+
+        b_k = keep.tile([P, E, HALVES * ROWS, P], BF16)
+        for e in range(E):
+            b_t = flip.tile([P, HALVES * ROWS, P], BF16, tag="flip")
+            for s in range(HALVES):
+                for j in range(ROWS):
+                    nc.tensor.transpose(
+                        b_t[:, s * ROWS + j, :], b_sb[:, e, s, j * R : (j + 1) * R], ident_bf16[:]
+                    )
+            nc.scalar.copy(out=b_k[:, e], in_=b_t[:])
+
+        delta = keep.tile([P, E, HALVES, ROWS, T], F32)
+        for e in range(E):
+            for s in range(HALVES):
+                delta_ps = sums.tile([P, ROWS, T], F32, tag="sums")
+                for j in range(ROWS):
+                    nc.tensor.matmul(
+                        delta_ps[:, j, :],
+                        lhsT=b_k[:, e, s * ROWS + j, :],
+                        rhs=low_k[:, e, :],
+                        start=True,
+                        stop=True,
+                    )
+                if s == 0:
+                    nc.scalar.copy(out=delta[:, e, s], in_=delta_ps[:])
+                else:
+                    nc.vector.tensor_copy(out=delta[:, e, s], in_=delta_ps[:])
+
+        x_words = x_sb[:].bitcast(F32)
+        x_t = flip.tile([P, E, PAIR, T], F32, tag="flip")
+        for e in range(E):
+            for u in range(PAIR):
+                nc.tensor.transpose(x_t[:, e, u, :], x_words[:, e, u * P : (u + 1) * P], ident_f32[:])
+        x_grouped = keep.tile([P, E, T, PACK], BF16, align_bytes=64)
+        nc.vector.tensor_copy(out=x_grouped[:].bitcast(F32), in_=x_t[:].rearrange("q e u t -> q e t u"))
+        x_codes = keep.tile([P, E * T], U32, align_bytes=64)
+        x_scales = keep.tile([P, E * T], U8, align_bytes=64)
+        nc.vector.quantize_mx(
+            out=x_codes[:].bitcast(FP8X4),
+            scales=x_scales[:],
+            in_=x_grouped[:].rearrange("q e t k -> q (e t k)"),
+        )
+
+        w_grouped = {}
+        w_codes = {}
+        w_scales = {}
+        gate_act = {}
+        h_f32 = {}
+        h_grouped = {}
+
+        def flip_piece(i):
+            words = w_raw[i][:].bitcast(F32)
+            w_t = flip.tile([P, J, PAIR, P], F32, tag="flip")
+            for j in range(J):
+                for u in range(PAIR):
+                    first = (j * PAIR + u) * P
+                    nc.tensor.transpose(w_t[:, j, u, :], words[:, first : first + P], ident_f32[:])
+            grouped = work.tile([P, J, P, PACK], BF16, align_bytes=64, name="w_grouped")
+            nc.scalar.copy(out=grouped[:].bitcast(F32), in_=w_t[:].rearrange("q j u p -> q j p u"))
+            w_grouped[i] = grouped
+
+        def quantise_piece(i):
+            codes = work.tile([P, J * P], U32, align_bytes=64, name="w_codes")
+            scales = work.tile([P, J * P], U8, align_bytes=64, name="w_scales")
+            nc.vector.quantize_mx(
+                out=codes[:].bitcast(FP8X4),
+                scales=scales[:],
+                in_=w_grouped[i][:].rearrange("q j p k -> q (j p k)"),
+            )
+            w_codes[i] = codes
+            w_scales[i] = scales
+
+        def multiply_piece(i):
+            e, a, s = pieces[i]
+            base = sums.tile([P, J, T], F32, tag="sums")
+            for j in range(J):
+                nc.tensor.matmul_mx(
+                    out=base[:, j, :],
+                    lhsT=w_codes[i][:, j * P : (j + 1) * P].bitcast(FP8X4),
+                    lhsT_scale=w_scales[i][:, j * P : (j + 1) * P],
+                    rhs=x_codes[:, e * T : (e + 1) * T].bitcast(FP8X4),
+                    rhs_scale=x_scales[:, e * T : (e + 1) * T],
+                    start=True,
+                    stop=True,
+                )
+            rows = slice(a * J, (a + 1) * J)
+            total = work.tile([P, J, T], F32, name="total")
+            nc.vector.scalar_tensor_tensor(
+                out=total[:],
+                in0=delta[:, e, s, rows, :],
+                scalar=LORA_SCALE,
+                in1=base[:],
+                op0=ALU.mult,
+                op1=ALU.add,
+            )
+            if s == 0:
+                act = work.tile([P, J, T], F32, name="gate_act")
+                nc.scalar.activation(out=act[:], in_=total[:], func=ACT.Silu)
+                gate_act[(e, a)] = act
+                return
+            if a == 0:
+                h_f32[e] = keep.tile([P, ROWS, T], F32, name="h_f32_%d" % e)
+                h_grouped[e] = keep.tile([P, T, PACK], BF16, align_bytes=64, name="h_grouped_%d" % e)
+            nc.vector.tensor_tensor(out=h_f32[e][:, rows, :], in0=total[:], in1=gate_act[(e, a)][:], op=ALU.mult)
+            nc.scalar.copy(
+                out=h_grouped[e][:, :, rows], in_=h_f32[e][:, rows, :].rearrange("p j t -> p t j")
+            )
+
+        def store_h(e):
+            h_t = flip.tile([P, ROWS, P], F32, tag="flip")
+            for j in range(ROWS):
+                nc.tensor.transpose(h_t[:, j, :], h_f32[e][:, j, :], ident_f32[:])
+            h_out = work.tile([P, P, ROWS], F32, name="h_out")
+            nc.scalar.copy(out=h_out[:], in_=h_t[:].rearrange("t j p -> t p j"))
+            nc.sync.dma_start(out=out_0[e], in_=h_out[:].rearrange("t p j -> t (p j)"))
+
+        AHEAD = 2
+        for i in range(len(pieces) + AHEAD):
+            if i < len(pieces):
+                flip_piece(i)
+            if 1 <= i <= len(pieces):
+                quantise_piece(i - 1)
+            if i >= AHEAD:
+                multiply_piece(i - AHEAD)
+                e, a, s = pieces[i - AHEAD]
+                if a == STEPS - 1 and s == HALVES - 1:
+                    store_h(e)
+
+        a_words = a_sb[:].bitcast(F32).rearrange("r e (q u) -> r e u q", u=PAIR)
+        a_t = flip.tile([P, E, PAIR, R], F32, tag="flip")
+        for e in range(E):
+            for u in range(PAIR):
+                nc.tensor.transpose(a_t[:, e, u, :], a_words[:, e, u, :], ident_f32[:])
+        a_grouped = keep.tile([P, E, R, PACK], BF16, align_bytes=64)
+        nc.vector.tensor_copy(out=a_grouped[:].bitcast(F32), in_=a_t[:].rearrange("q e u r -> q e r u"))
+        a_codes = keep.tile([P, E * R], U32, align_bytes=64)
+        a_scales = keep.tile([P, E * R], U8, align_bytes=64)
+        nc.vector.quantize_mx(
+            out=a_codes[:].bitcast(FP8X4),
+            scales=a_scales[:],
+            in_=a_grouped[:].rearrange("q e r k -> q (e r k)"),
+        )
+
+        for e in range(E):
+            h_codes = work.tile([P, T], U32, align_bytes=64, name="h_codes")
+            h_scales = work.tile([P, T], U8, align_bytes=64, name="h_scales")
+            nc.vector.quantize_mx(
+                out=h_codes[:].bitcast(FP8X4),
+                scales=h_scales[:],
+                in_=h_grouped[e][:].rearrange("p t k -> p (t k)"),
+            )
+            low_d_ps = last.tile([P, R], F32)
+            nc.tensor.matmul_mx(
+                out=low_d_ps[:],
+                lhsT=h_codes[:].bitcast(FP8X4),
+                lhsT_scale=h_scales[:],
+                rhs=a_codes[:, e * R : (e + 1) * R].bitcast(FP8X4),
+                rhs_scale=a_scales[:, e * R : (e + 1) * R],
+                start=True,
+                stop=True,
+            )
+            low_d_sb = work.tile([P, R], F32, name="low_d_sb")
+            nc.vector.tensor_copy(out=low_d_sb[:], in_=low_d_ps[:])
+            nc.sync.dma_start(out=out_1[e], in_=low_d_sb[:])

@@ -16,46 +16,47 @@ LORA_SCALE = 2.0
 P = 128
 PACK = 4
 PAIR = 2
+GATE, UP = 0, 1
 HALVES = 2
-ROWS = D // P
 STEPS = 2
-J = ROWS // STEPS
+J = D // (STEPS * P)
 
 FLOPS = 2 * E * T * (H * 2 * D + R * 2 * D + D * R)
 
 
 def tile_loralinearexpertswrapper_pa_s_kernel(tc, x, low_gu, W_gu, B_gu, A_d, out_0, out_1):
     nc = tc.nc
+    steps = [(e, a) for e in range(E) for a in range(STEPS)]
+    n_steps = len(steps)
     with ExitStack() as ctx:
+        ctx.enter_context(tc.manual_schedule())
         keep = ctx.enter_context(tc.tile_pool(name="keep", bufs=1))
-        w_pool = ctx.enter_context(tc.tile_pool(name="w_pool", bufs=E * STEPS * HALVES))
-        work = ctx.enter_context(tc.tile_pool(name="work", bufs=3))
-        flip = ctx.enter_context(tc.psum_pool(name="flip", bufs=3))
-        sums = ctx.enter_context(tc.psum_pool(name="sums", bufs=4))
+        work = ctx.enter_context(tc.tile_pool(name="work", bufs=4))
+        flip = ctx.enter_context(tc.psum_pool(name="flip", bufs=4))
+        sums = ctx.enter_context(tc.psum_pool(name="sums", bufs=3))
         last = ctx.enter_context(tc.psum_pool(name="last", bufs=1))
 
         low_sb = keep.tile([P, E, R], BF16)
         nc.sync.dma_start(out=low_sb[:], in_=low_gu.rearrange("e t r -> t e r"))
-        b_sb = keep.tile([P, E, HALVES, ROWS * R], BF16)
-        b_rows = B_gu.rearrange("e (s p j) r -> e p s (j r)", s=HALVES, p=P)
+        b_sb = keep.tile([P, E, HALVES * STEPS, J * R], BF16)
+        b_rows = B_gu.rearrange("e (c p j) r -> e p c (j r)", c=HALVES * STEPS, p=P)
         for e in range(E):
             nc.sync.dma_start(out=b_sb[:, e], in_=b_rows[e])
         x_sb = keep.tile([P, E, H], BF16)
         nc.sync.dma_start(out=x_sb[:], in_=x.rearrange("e t h -> t e h"))
-        pieces = [(e, a, s) for e in range(E) for a in range(STEPS) for s in range(HALVES)]
-        w_rows = W_gu.rearrange("e (s p a j) h -> e a s p (j h)", s=HALVES, p=P, a=STEPS)
-        w_raw = []
-        for e, a, s in pieces:
-            raw = w_pool.tile([P, J * H], BF16, name="w_raw")
-            nc.sync.dma_start(out=raw[:], in_=w_rows[e, a, s])
-            w_raw.append(raw)
+        w_rows = W_gu.rearrange("e (s a p j) h -> e a s p (j h)", s=HALVES, a=STEPS, p=P)
+        w_sb = {}
+        for k, (e, a) in enumerate(steps):
+            for s in range(HALVES):
+                w_sb[(k, s)] = keep.tile([P, J * H], BF16, name="w_sb_%d_%d" % (k, s))
+                nc.sync.dma_start(out=w_sb[(k, s)][:], in_=w_rows[e, a, s])
         a_sb = keep.tile([P, E, D], BF16)
         nc.sync.dma_start(out=a_sb[:], in_=A_d.rearrange("e r d -> r e d"))
 
-        ident_f32 = keep.tile([P, P], F32)
-        make_identity(nc, ident_f32[:])
         ident_bf16 = keep.tile([P, P], BF16)
         make_identity(nc, ident_bf16[:])
+        ident_f32 = keep.tile([P, P], F32)
+        make_identity(nc, ident_f32[:])
         zero = keep.tile([P, 1], F32)
         nc.vector.memset(zero[:], 0.0)
         unused = keep.tile([P, 1], F32)
@@ -67,40 +68,45 @@ def tile_loralinearexpertswrapper_pa_s_kernel(tc, x, low_gu, W_gu, B_gu, A_d, ou
         low_k = keep.tile([P, E, T], BF16)
         nc.scalar.copy(out=low_k[:], in_=low_t[:])
 
-        b_k = keep.tile([P, E, HALVES * ROWS, P], BF16)
+        b_k = keep.tile([P, E, HALVES * STEPS * J, P], BF16)
         for e in range(E):
-            b_t = flip.tile([P, HALVES * ROWS, P], BF16, tag="flip")
-            for s in range(HALVES):
-                for j in range(ROWS):
-                    nc.tensor.transpose(
-                        b_t[:, s * ROWS + j, :], b_sb[:, e, s, j * R : (j + 1) * R], ident_bf16[:]
-                    )
+            b_t = flip.tile([P, HALVES * STEPS * J, P], BF16, tag="flip")
+            for c in range(HALVES * STEPS):
+                for j in range(J):
+                    nc.tensor.transpose(b_t[:, c * J + j, :], b_sb[:, e, c, j * R : (j + 1) * R], ident_bf16[:])
             nc.scalar.copy(out=b_k[:, e], in_=b_t[:])
 
-        delta = keep.tile([P, E, HALVES, ROWS, T], F32)
-        for e in range(E):
+        delta = keep.tile([P, E, HALVES, STEPS, J, T], F32)
+
+        def lora_term(e):
             for s in range(HALVES):
-                delta_ps = sums.tile([P, ROWS, T], F32, tag="sums")
-                for j in range(ROWS):
+                delta_ps = sums.tile([P, STEPS * J, T], F32, tag="sums")
+                for c in range(STEPS * J):
                     nc.tensor.matmul(
-                        delta_ps[:, j, :],
-                        lhsT=b_k[:, e, s * ROWS + j, :],
+                        delta_ps[:, c, :],
+                        lhsT=b_k[:, e, s * STEPS * J + c, :],
                         rhs=low_k[:, e, :],
                         start=True,
                         stop=True,
                     )
-                if s == 0:
-                    nc.scalar.copy(out=delta[:, e, s], in_=delta_ps[:])
+                flat = delta[:, e, s].rearrange("p a j t -> p (a j) t")
+                if s == GATE:
+                    nc.scalar.copy(out=flat, in_=delta_ps[:])
                 else:
-                    nc.vector.tensor_copy(out=delta[:, e, s], in_=delta_ps[:])
+                    nc.vector.tensor_copy(out=flat, in_=delta_ps[:])
 
+        def transpose_words(out, words):
+            for u in range(PAIR):
+                nc.tensor.transpose(out[:, u, :], words[:, u * P : (u + 1) * P], ident_f32[:])
+
+        lora_term(0)
         x_words = x_sb[:].bitcast(F32)
         x_t = flip.tile([P, E, PAIR, T], F32, tag="flip")
         for e in range(E):
-            for u in range(PAIR):
-                nc.tensor.transpose(x_t[:, e, u, :], x_words[:, e, u * P : (u + 1) * P], ident_f32[:])
+            transpose_words(x_t[:, e], x_words[:, e, :])
         x_grouped = keep.tile([P, E, T, PACK], BF16, align_bytes=64)
         nc.vector.tensor_copy(out=x_grouped[:].bitcast(F32), in_=x_t[:].rearrange("q e u t -> q e t u"))
+        lora_term(1)
         x_codes = keep.tile([P, E * T], U32, align_bytes=64)
         x_scales = keep.tile([P, E * T], U8, align_bytes=64)
         nc.vector.quantize_mx(
@@ -109,124 +115,157 @@ def tile_loralinearexpertswrapper_pa_s_kernel(tc, x, low_gu, W_gu, B_gu, A_d, ou
             in_=x_grouped[:].rearrange("q e t k -> q (e t k)"),
         )
 
+        w_t = {}
         w_grouped = {}
         w_codes = {}
         w_scales = {}
+        base = {}
+        total = {}
         gate_act = {}
         h_f32 = {}
-        h_grouped = {}
+        h_t = {}
+        h_grouped = keep.tile([P, E, T, PACK], BF16, align_bytes=64)
+        h_codes = keep.tile([P, E * T], U32, align_bytes=64)
+        h_scales = keep.tile([P, E * T], U8, align_bytes=64)
 
-        def flip_piece(i):
-            words = w_raw[i][:].bitcast(F32)
-            w_t = flip.tile([P, J, PAIR, P], F32, tag="flip")
+        def transpose_w(k, s):
+            words = w_sb[(k, s)][:].bitcast(F32).rearrange("p (j w) -> p j w", j=J)
+            w_t[(k, s)] = flip.tile([P, J, PAIR, P], F32, tag="flip", name="w_t")
             for j in range(J):
-                for u in range(PAIR):
-                    first = (j * PAIR + u) * P
-                    nc.tensor.transpose(w_t[:, j, u, :], words[:, first : first + P], ident_f32[:])
-            grouped = work.tile([P, J, P, PACK], BF16, align_bytes=64, name="w_grouped")
-            nc.scalar.copy(out=grouped[:].bitcast(F32), in_=w_t[:].rearrange("q j u p -> q j p u"))
-            w_grouped[i] = grouped
+                transpose_words(w_t[(k, s)][:, j], words[:, j, :])
 
-        def quantise_piece(i):
-            codes = work.tile([P, J * P], U32, align_bytes=64, name="w_codes")
-            scales = work.tile([P, J * P], U8, align_bytes=64, name="w_scales")
-            nc.vector.quantize_mx(
-                out=codes[:].bitcast(FP8X4),
-                scales=scales[:],
-                in_=w_grouped[i][:].rearrange("q j p k -> q (j p k)"),
+        def regroup_w(k, s):
+            w_grouped[(k, s)] = work.tile([P, J, P, PACK], BF16, align_bytes=64, name="w_grouped")
+            nc.scalar.copy(
+                out=w_grouped[(k, s)][:].bitcast(F32), in_=w_t[(k, s)][:].rearrange("q j u p -> q j p u")
             )
-            w_codes[i] = codes
-            w_scales[i] = scales
 
-        def multiply_piece(i):
-            e, a, s = pieces[i]
-            base = sums.tile([P, J, T], F32, tag="sums")
-            for j in range(J):
-                nc.tensor.matmul_mx(
-                    out=base[:, j, :],
-                    lhsT=w_codes[i][:, j * P : (j + 1) * P].bitcast(FP8X4),
-                    lhsT_scale=w_scales[i][:, j * P : (j + 1) * P],
-                    rhs=x_codes[:, e * T : (e + 1) * T].bitcast(FP8X4),
-                    rhs_scale=x_scales[:, e * T : (e + 1) * T],
-                    start=True,
-                    stop=True,
-                )
-            rows = slice(a * J, (a + 1) * J)
-            total = work.tile([P, J, T], F32, name="total")
+        def quantise_w(k, s):
+            w_codes[(k, s)] = work.tile([P, J * P], U32, align_bytes=64, name="w_codes")
+            w_scales[(k, s)] = work.tile([P, J * P], U8, align_bytes=64, name="w_scales")
+            nc.vector.quantize_mx(
+                out=w_codes[(k, s)][:].bitcast(FP8X4),
+                scales=w_scales[(k, s)][:],
+                in_=w_grouped[(k, s)][:].rearrange("q j p k -> q (j p k)"),
+            )
+
+        def multiply(k):
+            e = steps[k][0]
+            for s in range(HALVES):
+                base[(k, s)] = sums.tile([P, J, T], F32, tag="sums", name="base")
+                for j in range(J):
+                    nc.tensor.matmul_mx(
+                        out=base[(k, s)][:, j, :],
+                        lhsT=w_codes[(k, s)][:, j * P : (j + 1) * P].bitcast(FP8X4),
+                        lhsT_scale=w_scales[(k, s)][:, j * P : (j + 1) * P],
+                        rhs=x_codes[:, e * T : (e + 1) * T].bitcast(FP8X4),
+                        rhs_scale=x_scales[:, e * T : (e + 1) * T],
+                        start=True,
+                        stop=True,
+                    )
+
+        def add_lora(k, s):
+            e, a = steps[k]
+            total[(k, s)] = work.tile([P, J, T], F32, name="total")
             nc.vector.scalar_tensor_tensor(
-                out=total[:],
-                in0=delta[:, e, s, rows, :],
+                out=total[(k, s)][:],
+                in0=delta[:, e, s, a],
                 scalar=LORA_SCALE,
-                in1=base[:],
+                in1=base[(k, s)][:],
                 op0=ALU.mult,
                 op1=ALU.add,
             )
-            if s == 0:
-                act = work.tile([P, J, T], F32, name="gate_act")
-                nc.scalar.activation(out=act[:], in_=total[:], func=ACT.Silu)
-                gate_act[(e, a)] = act
-                return
-            if a == 0:
-                h_f32[e] = keep.tile([P, ROWS, T], F32, name="h_f32_%d" % e)
-                h_grouped[e] = keep.tile([P, T, PACK], BF16, align_bytes=64, name="h_grouped_%d" % e)
-            nc.vector.tensor_tensor(out=h_f32[e][:, rows, :], in0=total[:], in1=gate_act[(e, a)][:], op=ALU.mult)
-            nc.scalar.copy(
-                out=h_grouped[e][:, :, rows], in_=h_f32[e][:, rows, :].rearrange("p j t -> p t j")
+
+        def silu_gate(k):
+            gate_act[k] = work.tile([P, J, T], F32, name="gate_act")
+            nc.scalar.activation(out=gate_act[k][:], in_=total[(k, GATE)][:], func=ACT.Silu)
+
+        def product(k):
+            h_f32[k] = work.tile([P, J, T], F32, name="h_f32")
+            nc.vector.tensor_tensor(out=h_f32[k][:], in0=total[(k, UP)][:], in1=gate_act[k][:], op=ALU.mult)
+            h_t[k] = flip.tile([P, J, P], F32, tag="flip", name="h_t")
+            for j in range(J):
+                nc.tensor.transpose(h_t[k][:, j, :], h_f32[k][:, j, :], ident_f32[:])
+
+        def round_h(k):
+            e, a = steps[k]
+            nc.vector.tensor_copy(
+                out=h_grouped[:, e, :, a * J : (a + 1) * J], in_=h_f32[k][:].rearrange("p j t -> p t j")
             )
 
-        def store_h(e):
-            h_t = flip.tile([P, ROWS, P], F32, tag="flip")
-            for j in range(ROWS):
-                nc.tensor.transpose(h_t[:, j, :], h_f32[e][:, j, :], ident_f32[:])
-            h_out = work.tile([P, P, ROWS], F32, name="h_out")
-            nc.scalar.copy(out=h_out[:], in_=h_t[:].rearrange("t j p -> t p j"))
-            nc.sync.dma_start(out=out_0[e], in_=h_out[:].rearrange("t p j -> t (p j)"))
+        def quantise_h(e):
+            nc.vector.quantize_mx(
+                out=h_codes[:, e * T : (e + 1) * T].bitcast(FP8X4),
+                scales=h_scales[:, e * T : (e + 1) * T],
+                in_=h_grouped[:, e].rearrange("p t k -> p (t k)"),
+            )
 
-        AHEAD = 2
-        for i in range(len(pieces) + AHEAD):
-            if i < len(pieces):
-                flip_piece(i)
-            if 1 <= i <= len(pieces):
-                quantise_piece(i - 1)
-            if i >= AHEAD:
-                multiply_piece(i - AHEAD)
-                e, a, s = pieces[i - AHEAD]
-                if a == STEPS - 1 and s == HALVES - 1:
-                    store_h(e)
+        def store_h(k):
+            e, a = steps[k]
+            h_out = work.tile([P, P, J], F32, name="h_out")
+            nc.scalar.copy(out=h_out[:], in_=h_t[k][:].rearrange("t j p -> t p j"))
+            nc.sync.dma_start(
+                out=out_0[e][:, a * J * P : (a + 1) * J * P], in_=h_out[:].rearrange("t p j -> t (p j)")
+            )
 
-        a_words = a_sb[:].bitcast(F32).rearrange("r e (q u) -> r e u q", u=PAIR)
-        a_t = flip.tile([P, E, PAIR, R], F32, tag="flip")
-        for e in range(E):
-            for u in range(PAIR):
-                nc.tensor.transpose(a_t[:, e, u, :], a_words[:, e, u, :], ident_f32[:])
         a_grouped = keep.tile([P, E, R, PACK], BF16, align_bytes=64)
-        nc.vector.tensor_copy(out=a_grouped[:].bitcast(F32), in_=a_t[:].rearrange("q e u r -> q e r u"))
         a_codes = keep.tile([P, E * R], U32, align_bytes=64)
         a_scales = keep.tile([P, E * R], U8, align_bytes=64)
-        nc.vector.quantize_mx(
-            out=a_codes[:].bitcast(FP8X4),
-            scales=a_scales[:],
-            in_=a_grouped[:].rearrange("q e r k -> q (e r k)"),
-        )
 
-        for e in range(E):
-            h_codes = work.tile([P, T], U32, align_bytes=64, name="h_codes")
-            h_scales = work.tile([P, T], U8, align_bytes=64, name="h_scales")
+        def transpose_a():
+            a_words = a_sb[:].bitcast(F32)
+            a_t = flip.tile([P, E, PAIR, R], F32, tag="flip")
+            for e in range(E):
+                transpose_words(a_t[:, e], a_words[:, e, :])
+            nc.scalar.copy(out=a_grouped[:].bitcast(F32), in_=a_t[:].rearrange("q e u r -> q e r u"))
+
+        def quantise_a():
             nc.vector.quantize_mx(
-                out=h_codes[:].bitcast(FP8X4),
-                scales=h_scales[:],
-                in_=h_grouped[e][:].rearrange("p t k -> p (t k)"),
+                out=a_codes[:].bitcast(FP8X4),
+                scales=a_scales[:],
+                in_=a_grouped[:].rearrange("q e r k -> q (e r k)"),
             )
-            low_d_ps = last.tile([P, R], F32)
+
+        for b in range(-1, n_steps + 2):
+            if b + 1 < n_steps:
+                transpose_w(b + 1, GATE)
+                transpose_w(b + 1, UP)
+                regroup_w(b + 1, GATE)
+                regroup_w(b + 1, UP)
+            if b + 1 == n_steps:
+                transpose_a()
+            if 0 <= b < n_steps:
+                quantise_w(b, GATE)
+            if 0 <= b - 2 < n_steps:
+                round_h(b - 2)
+            if 0 <= b - 1 < n_steps:
+                add_lora(b - 1, GATE)
+                silu_gate(b - 1)
+            if 0 <= b - 2 < n_steps and steps[b - 2][1] == STEPS - 1:
+                quantise_h(steps[b - 2][0])
+            if 0 <= b - 1 < n_steps:
+                add_lora(b - 1, UP)
+            if 0 <= b < n_steps:
+                quantise_w(b, UP)
+                multiply(b)
+            if b == n_steps:
+                quantise_a()
+            if 0 <= b - 1 < n_steps:
+                product(b - 1)
+            if 0 <= b - 2 < n_steps:
+                store_h(b - 2)
+
+        low_d_ps = last.tile([P, E, R], F32)
+        for e in range(E):
             nc.tensor.matmul_mx(
-                out=low_d_ps[:],
-                lhsT=h_codes[:].bitcast(FP8X4),
-                lhsT_scale=h_scales[:],
+                out=low_d_ps[:, e, :],
+                lhsT=h_codes[:, e * T : (e + 1) * T].bitcast(FP8X4),
+                lhsT_scale=h_scales[:, e * T : (e + 1) * T],
                 rhs=a_codes[:, e * R : (e + 1) * R].bitcast(FP8X4),
                 rhs_scale=a_scales[:, e * R : (e + 1) * R],
                 start=True,
                 stop=True,
             )
-            low_d_sb = work.tile([P, R], F32, name="low_d_sb")
-            nc.vector.tensor_copy(out=low_d_sb[:], in_=low_d_ps[:])
-            nc.sync.dma_start(out=out_1[e], in_=low_d_sb[:])
+        low_d_sb = keep.tile([P, E, R], F32)
+        nc.vector.tensor_copy(out=low_d_sb[:], in_=low_d_ps[:])
+        nc.sync.dma_start(out=out_1.rearrange("e t r -> t e r"), in_=low_d_sb[:])

@@ -29,7 +29,6 @@ def tile_loralinearexpertswrapper_pa_s_kernel(tc, x, low_gu, W_gu, B_gu, A_d, ou
     steps = [(e, a) for e in range(E) for a in range(STEPS)]
     n_steps = len(steps)
     with ExitStack() as ctx:
-        ctx.enter_context(tc.manual_schedule())
         keep = ctx.enter_context(tc.tile_pool(name="keep", bufs=1))
         work = ctx.enter_context(tc.tile_pool(name="work", bufs=4))
         flip = ctx.enter_context(tc.psum_pool(name="flip", bufs=4))

@@ -7,6 +7,7 @@ F32 = mybir.dt.float32
 BF16 = mybir.dt.bfloat16
 U32 = mybir.dt.uint32
 U8 = mybir.dt.uint8
+I32 = mybir.dt.int32
 FP8X4 = mybir.dt.float8_e4m3fn_x4
 ACT = mybir.ActivationFunctionType
 ALU = mybir.AluOpType
@@ -20,6 +21,8 @@ GATE, UP = 0, 1
 HALVES = 2
 STEPS = 2
 J = D // (STEPS * P)
+WARM_PASSES = 8
+WARM_N = 256
 
 FLOPS = 2 * E * T * (H * 2 * D + R * 2 * D + D * R)
 
@@ -60,6 +63,23 @@ def tile_loralinearexpertswrapper_pa_s_kernel(tc, x, low_gu, W_gu, B_gu, A_d, ou
         nc.vector.memset(zero[:], 0.0)
         unused = keep.tile([P, 1], F32)
         nc.scalar.activation(out=unused[:], in_=zero[:], func=ACT.Silu)
+
+        zeros = keep.tile([P, WARM_N * PACK], BF16, align_bytes=64)
+        nc.vector.memset(zeros[:].bitcast(I32), 0)
+        zero_codes = keep.tile([P, WARM_N], U32, align_bytes=64)
+        zero_scales = keep.tile([P, WARM_N], U8, align_bytes=64)
+        nc.vector.quantize_mx(out=zero_codes[:].bitcast(FP8X4), scales=zero_scales[:], in_=zeros[:])
+        warm_ps = last.tile([P, WARM_N], F32, tag="last")
+        for i in range(WARM_PASSES):
+            nc.tensor.matmul_mx(
+                out=warm_ps[:],
+                lhsT=zero_codes[:, :P].bitcast(FP8X4),
+                lhsT_scale=zero_scales[:, :P],
+                rhs=zero_codes[:].bitcast(FP8X4),
+                rhs_scale=zero_scales[:],
+                start=True,
+                stop=True,
+            )
 
         low_t = flip.tile([P, E, T], BF16, tag="flip")
         for e in range(E):
@@ -254,7 +274,7 @@ def tile_loralinearexpertswrapper_pa_s_kernel(tc, x, low_gu, W_gu, B_gu, A_d, ou
             if 0 <= b - 2 < n_steps:
                 store_h(b - 2)
 
-        low_d_ps = last.tile([P, E, R], F32)
+        low_d_ps = last.tile([P, E, R], F32, tag="last")
         for e in range(E):
             nc.tensor.matmul_mx(
                 out=low_d_ps[:, e, :],

@@ -21,7 +21,8 @@ GATE, UP = 0, 1
 HALVES = 2
 STEPS = 2
 J = D // (STEPS * P)
-WARM_PASSES = 8
+DS = J * P
+WARM_PASSES = 3
 WARM_N = 256
 
 FLOPS = 2 * E * T * (H * 2 * D + R * 2 * D + D * R)
@@ -35,25 +36,39 @@ def tile_loralinearexpertswrapper_pa_s_kernel(tc, x, low_gu, W_gu, B_gu, A_d, ou
         keep = ctx.enter_context(tc.tile_pool(name="keep", bufs=1))
         work = ctx.enter_context(tc.tile_pool(name="work", bufs=4))
         flip = ctx.enter_context(tc.psum_pool(name="flip", bufs=4))
-        sums = ctx.enter_context(tc.psum_pool(name="sums", bufs=3))
-        last = ctx.enter_context(tc.psum_pool(name="last", bufs=1))
+        sums = ctx.enter_context(tc.psum_pool(name="sums", bufs=4))
+        ctx.enter_context(tc.manual_schedule())
 
         low_sb = keep.tile([P, E, R], BF16)
         nc.sync.dma_start(out=low_sb[:], in_=low_gu.rearrange("e t r -> t e r"))
-        b_sb = keep.tile([P, E, HALVES * STEPS, J * R], BF16)
-        b_rows = B_gu.rearrange("e (c p j) r -> e p c (j r)", c=HALVES * STEPS, p=P)
-        for e in range(E):
-            nc.sync.dma_start(out=b_sb[:, e], in_=b_rows[e])
+        b_rows = B_gu.rearrange("e (s a p j) r -> e a p s (j r)", s=HALVES, a=STEPS, p=P)
+        b_sb = {}
+
+        def load_b(e, a):
+            b_sb[(e, a)] = keep.tile([P, HALVES, J * R], BF16, name="b_sb_%d_%d" % (e, a))
+            nc.sync.dma_start(out=b_sb[(e, a)][:], in_=b_rows[e, a])
+
         x_sb = keep.tile([P, E, H], BF16)
-        nc.sync.dma_start(out=x_sb[:], in_=x.rearrange("e t h -> t e h"))
+        a_sb = keep.tile([P, E, D], BF16)
         w_rows = W_gu.rearrange("e (s a p j) h -> e a s p (j h)", s=HALVES, a=STEPS, p=P)
         w_sb = {}
-        for k, (e, a) in enumerate(steps):
+
+        def load_w(k):
+            e, a = steps[k]
             for s in range(HALVES):
                 w_sb[(k, s)] = keep.tile([P, J * H], BF16, name="w_sb_%d_%d" % (k, s))
                 nc.sync.dma_start(out=w_sb[(k, s)][:], in_=w_rows[e, a, s])
-        a_sb = keep.tile([P, E, D], BF16)
+
+        load_b(0, 0)
+        load_b(0, 1)
+        nc.sync.dma_start(out=x_sb[:], in_=x.rearrange("e t h -> t e h"))
+        load_w(0)
+        load_w(1)
+        load_b(1, 0)
+        load_b(1, 1)
+        load_w(2)
         nc.sync.dma_start(out=a_sb[:], in_=A_d.rearrange("e r d -> r e d"))
+        load_w(3)
 
         ident_bf16 = keep.tile([P, P], BF16)
         make_identity(nc, ident_bf16[:])
@@ -69,7 +84,7 @@ def tile_loralinearexpertswrapper_pa_s_kernel(tc, x, low_gu, W_gu, B_gu, A_d, ou
         zero_codes = keep.tile([P, WARM_N], U32, align_bytes=64)
         zero_scales = keep.tile([P, WARM_N], U8, align_bytes=64)
         nc.vector.quantize_mx(out=zero_codes[:].bitcast(FP8X4), scales=zero_scales[:], in_=zeros[:])
-        warm_ps = last.tile([P, WARM_N], F32, tag="last")
+        warm_ps = sums.tile([P, WARM_N], F32, tag="sums")
         for i in range(WARM_PASSES):
             nc.tensor.matmul_mx(
                 out=warm_ps[:],
@@ -81,58 +96,66 @@ def tile_loralinearexpertswrapper_pa_s_kernel(tc, x, low_gu, W_gu, B_gu, A_d, ou
                 stop=True,
             )
 
-        low_t = flip.tile([P, E, T], BF16, tag="flip")
-        for e in range(E):
-            nc.tensor.transpose(low_t[:, e, :], low_sb[:, e, :], ident_bf16[:])
+        def transpose_low():
+            low_t = flip.tile([P, E, T], BF16, tag="flip", name="low_t")
+            for e in range(E):
+                nc.tensor.transpose(low_t[:, e, :], low_sb[:, e, :], ident_bf16[:])
+            nc.scalar.copy(out=low_k[:], in_=low_t[:])
+
         low_k = keep.tile([P, E, T], BF16)
-        nc.scalar.copy(out=low_k[:], in_=low_t[:])
+        b_k = keep.tile([P, E, STEPS, J * HALVES, P], BF16)
+        delta = keep.tile([P, E, STEPS, J, HALVES, P], F32)
+        b_t = {}
 
-        b_k = keep.tile([P, E, HALVES * STEPS * J, P], BF16)
-        for e in range(E):
-            b_t = flip.tile([P, HALVES * STEPS * J, P], BF16, tag="flip")
-            for c in range(HALVES * STEPS):
-                for j in range(J):
-                    nc.tensor.transpose(b_t[:, c * J + j, :], b_sb[:, e, c, j * R : (j + 1) * R], ident_bf16[:])
-            nc.scalar.copy(out=b_k[:, e], in_=b_t[:])
-
-        delta = keep.tile([P, E, HALVES, STEPS, J, T], F32)
-
-        def lora_term(e):
-            for s in range(HALVES):
-                delta_ps = sums.tile([P, STEPS * J, T], F32, tag="sums")
-                for c in range(STEPS * J):
-                    nc.tensor.matmul(
-                        delta_ps[:, c, :],
-                        lhsT=b_k[:, e, s * STEPS * J + c, :],
-                        rhs=low_k[:, e, :],
-                        start=True,
-                        stop=True,
+        def transpose_b(e, a):
+            b_t[(e, a)] = flip.tile([P, J * HALVES, P], BF16, tag="flip", name="b_t")
+            for j in range(J):
+                for s in range(HALVES):
+                    nc.tensor.transpose(
+                        b_t[(e, a)][:, j * HALVES + s, :], b_sb[(e, a)][:, s, j * R : (j + 1) * R], ident_bf16[:]
                     )
-                flat = delta[:, e, s].rearrange("p a j t -> p (a j) t")
-                if s == GATE:
-                    nc.scalar.copy(out=flat, in_=delta_ps[:])
-                else:
-                    nc.vector.tensor_copy(out=flat, in_=delta_ps[:])
+
+        def copy_b(e, a):
+            nc.vector.tensor_copy(out=b_k[:, e, a], in_=b_t[(e, a)][:])
+
+        def lora_term(e, a):
+            delta_ps = sums.tile([P, J * HALVES, P], F32, tag="sums", name="delta_ps")
+            if (e, a) == steps[-1]:
+                for c in range(J * HALVES):
+                    nc.tensor.matmul(
+                        delta_ps[:, c, :], lhsT=b_k[:, e, a, c, :], rhs=low_k[:, e, :], start=True, stop=True
+                    )
+            else:
+                nc.tensor.matmul(
+                    delta_ps[:].rearrange("t c p -> t (c p)"),
+                    lhsT=low_k[:, e, :],
+                    rhs=b_k[:, e, a].rearrange("r c p -> r (c p)"),
+                    start=True,
+                    stop=True,
+                )
+            nc.scalar.copy(out=delta[:, e, a].rearrange("t j s p -> t (j s) p"), in_=delta_ps[:])
 
         def transpose_words(out, words):
             for u in range(PAIR):
                 nc.tensor.transpose(out[:, u, :], words[:, u * P : (u + 1) * P], ident_f32[:])
 
-        lora_term(0)
         x_words = x_sb[:].bitcast(F32)
-        x_t = flip.tile([P, E, PAIR, T], F32, tag="flip")
-        for e in range(E):
-            transpose_words(x_t[:, e], x_words[:, e, :])
         x_grouped = keep.tile([P, E, T, PACK], BF16, align_bytes=64)
-        nc.vector.tensor_copy(out=x_grouped[:].bitcast(F32), in_=x_t[:].rearrange("q e u t -> q e t u"))
-        lora_term(1)
         x_codes = keep.tile([P, E * T], U32, align_bytes=64)
         x_scales = keep.tile([P, E * T], U8, align_bytes=64)
-        nc.vector.quantize_mx(
-            out=x_codes[:].bitcast(FP8X4),
-            scales=x_scales[:],
-            in_=x_grouped[:].rearrange("q e t k -> q (e t k)"),
-        )
+
+        def transpose_x():
+            x_t = flip.tile([P, E, PAIR, T], F32, tag="flip")
+            for e in range(E):
+                transpose_words(x_t[:, e], x_words[:, e, :])
+            nc.vector.tensor_copy(out=x_grouped[:].bitcast(F32), in_=x_t[:].rearrange("q e u t -> q e t u"))
+
+        def quantise_x():
+            nc.vector.quantize_mx(
+                out=x_codes[:].bitcast(FP8X4),
+                scales=x_scales[:],
+                in_=x_grouped[:].rearrange("q e t k -> q (e t k)"),
+            )
 
         w_t = {}
         w_grouped = {}
@@ -147,84 +170,128 @@ def tile_loralinearexpertswrapper_pa_s_kernel(tc, x, low_gu, W_gu, B_gu, A_d, ou
         h_codes = keep.tile([P, E * T], U32, align_bytes=64)
         h_scales = keep.tile([P, E * T], U8, align_bytes=64)
 
-        def transpose_w(k, s):
-            words = w_sb[(k, s)][:].bitcast(F32).rearrange("p (j w) -> p j w", j=J)
-            w_t[(k, s)] = flip.tile([P, J, PAIR, P], F32, tag="flip", name="w_t")
-            for j in range(J):
-                transpose_words(w_t[(k, s)][:, j], words[:, j, :])
-
-        def regroup_w(k, s):
-            w_grouped[(k, s)] = work.tile([P, J, P, PACK], BF16, align_bytes=64, name="w_grouped")
-            nc.scalar.copy(
-                out=w_grouped[(k, s)][:].bitcast(F32), in_=w_t[(k, s)][:].rearrange("q j u p -> q j p u")
-            )
-
-        def quantise_w(k, s):
-            w_codes[(k, s)] = work.tile([P, J * P], U32, align_bytes=64, name="w_codes")
-            w_scales[(k, s)] = work.tile([P, J * P], U8, align_bytes=64, name="w_scales")
-            nc.vector.quantize_mx(
-                out=w_codes[(k, s)][:].bitcast(FP8X4),
-                scales=w_scales[(k, s)][:],
-                in_=w_grouped[(k, s)][:].rearrange("q j p k -> q (j p k)"),
-            )
-
-        def multiply(k):
-            e = steps[k][0]
+        def transpose_w(k, j):
+            w_t[(k, j)] = flip.tile([P, HALVES, PAIR, P], F32, tag="flip", name="w_t")
             for s in range(HALVES):
-                base[(k, s)] = sums.tile([P, J, T], F32, tag="sums", name="base")
-                for j in range(J):
+                words = w_sb[(k, s)][:].bitcast(F32).rearrange("p (j w) -> p j w", j=J)
+                transpose_words(w_t[(k, j)][:, s], words[:, j, :])
+
+        def regroup_w(k, j):
+            w_grouped[(k, j)] = work.tile([P, HALVES, P, PACK], BF16, align_bytes=64, name="w_grouped")
+            out = w_grouped[(k, j)][:].bitcast(F32)
+            in_ = w_t[(k, j)][:].rearrange("q s u p -> q s p u")
+            if (k, j) == (0, 1):
+                nc.vector.tensor_copy(out=out, in_=in_)
+            else:
+                nc.scalar.copy(out=out, in_=in_)
+
+        def quantise_w(k, j):
+            w_codes[(k, j)] = work.tile([P, HALVES * P], U32, align_bytes=64, name="w_codes")
+            w_scales[(k, j)] = work.tile([P, HALVES * P], U8, align_bytes=64, name="w_scales")
+            nc.vector.quantize_mx(
+                out=w_codes[(k, j)][:].bitcast(FP8X4),
+                scales=w_scales[(k, j)][:],
+                in_=w_grouped[(k, j)][:].rearrange("q s p k -> q (s p k)"),
+            )
+
+        def multiply(k, j):
+            e = steps[k][0]
+            x_c, x_s = x_codes[:, e * T : (e + 1) * T], x_scales[:, e * T : (e + 1) * T]
+            w_c, w_s = w_codes[(k, j)], w_scales[(k, j)]
+            if j == 0 or k == n_steps - 1:
+                base[(k, j)] = sums.tile([P, J, HALVES, P], F32, tag="sums", name="base")
+            else:
+                base[(k, j)] = base[(k, 0)]
+            if k == n_steps - 1:
+                for s in range(HALVES):
                     nc.tensor.matmul_mx(
-                        out=base[(k, s)][:, j, :],
-                        lhsT=w_codes[(k, s)][:, j * P : (j + 1) * P].bitcast(FP8X4),
-                        lhsT_scale=w_scales[(k, s)][:, j * P : (j + 1) * P],
-                        rhs=x_codes[:, e * T : (e + 1) * T].bitcast(FP8X4),
-                        rhs_scale=x_scales[:, e * T : (e + 1) * T],
+                        out=base[(k, j)][:, j, s, :],
+                        lhsT=w_c[:, s * P : (s + 1) * P].bitcast(FP8X4),
+                        lhsT_scale=w_s[:, s * P : (s + 1) * P],
+                        rhs=x_c.bitcast(FP8X4),
+                        rhs_scale=x_s,
                         start=True,
                         stop=True,
                     )
+            else:
+                nc.tensor.matmul_mx(
+                    out=base[(k, j)][:, j].rearrange("t s p -> t (s p)"),
+                    lhsT=x_c.bitcast(FP8X4),
+                    lhsT_scale=x_s,
+                    rhs=w_c[:].bitcast(FP8X4),
+                    rhs_scale=w_s[:],
+                    start=True,
+                    stop=True,
+                )
 
-        def add_lora(k, s):
+        def add_lora(k, js):
             e, a = steps[k]
-            total[(k, s)] = work.tile([P, J, T], F32, name="total")
+            if js.start == 0:
+                total[k] = work.tile([P, J, HALVES, P], F32, name="total")
             nc.vector.scalar_tensor_tensor(
-                out=total[(k, s)][:],
-                in0=delta[:, e, s, a],
+                out=total[k][:, js],
+                in0=delta[:, e, a, js],
                 scalar=LORA_SCALE,
-                in1=base[(k, s)][:],
+                in1=base[(k, js.start)][:, js],
                 op0=ALU.mult,
                 op1=ALU.add,
             )
 
-        def silu_gate(k):
-            gate_act[k] = work.tile([P, J, T], F32, name="gate_act")
-            nc.scalar.activation(out=gate_act[k][:], in_=total[(k, GATE)][:], func=ACT.Silu)
+        def silu_gate(k, js):
+            if js.start == 0:
+                gate_act[k] = work.tile([P, J, P], F32, name="gate_act")
+            nc.scalar.activation(out=gate_act[k][:, js], in_=total[k][:, js, GATE], func=ACT.Silu)
 
         def product(k):
-            h_f32[k] = work.tile([P, J, T], F32, name="h_f32")
-            nc.vector.tensor_tensor(out=h_f32[k][:], in0=total[(k, UP)][:], in1=gate_act[k][:], op=ALU.mult)
-            h_t[k] = flip.tile([P, J, P], F32, tag="flip", name="h_t")
+            h_f32[k] = work.tile([P, P, J], F32, name="h_f32")
+            nc.vector.tensor_tensor(
+                out=h_f32[k][:],
+                in0=total[k][:, :, UP].rearrange("t j p -> t p j"),
+                in1=gate_act[k][:].rearrange("t j p -> t p j"),
+                op=ALU.mult,
+            )
+
+        def store_h(k):
+            e, a = steps[k]
+            nc.sync.dma_start(out=out_0[e][:, a * DS : (a + 1) * DS], in_=h_f32[k][:].rearrange("t p j -> t (p j)"))
+
+        def transpose_h(k):
+            h_t[k] = flip.tile([P, J, T], F32, tag="flip", name="h_t")
             for j in range(J):
-                nc.tensor.transpose(h_t[k][:, j, :], h_f32[k][:, j, :], ident_f32[:])
+                nc.tensor.transpose(h_t[k][:, j, :], h_f32[k][:, :, j], ident_f32[:])
 
         def round_h(k):
             e, a = steps[k]
-            nc.vector.tensor_copy(
-                out=h_grouped[:, e, :, a * J : (a + 1) * J], in_=h_f32[k][:].rearrange("p j t -> p t j")
+            nc.scalar.copy(out=h_grouped[:, e, :, a * J : (a + 1) * J], in_=h_t[k][:].rearrange("p j t -> p t j"))
+
+        h_turned = keep.tile([P, J, T], F32)
+
+        def last_product(j):
+            k = n_steps - 1
+            nc.vector.tensor_tensor(
+                out=h_turned[:, j], in0=total[k][:, j, UP], in1=gate_act[k][:, j], op=ALU.mult
             )
+
+        def last_round():
+            e, a = steps[-1]
+            nc.vector.tensor_copy(
+                out=h_grouped[:, e, :, a * J : (a + 1) * J], in_=h_turned[:].rearrange("p j t -> p t j")
+            )
+
+        def last_transpose():
+            k = n_steps - 1
+            h_t[k] = flip.tile([P, J, P], F32, tag="flip", name="h_t")
+            for j in range(J):
+                nc.tensor.transpose(h_t[k][:, j, :], h_turned[:, j], ident_f32[:])
+            h_f32[k] = work.tile([P, P, J], F32, name="h_f32")
+            nc.scalar.copy(out=h_f32[k][:], in_=h_t[k][:].rearrange("t j p -> t p j"))
+            store_h(k)
 
         def quantise_h(e):
             nc.vector.quantize_mx(
                 out=h_codes[:, e * T : (e + 1) * T].bitcast(FP8X4),
                 scales=h_scales[:, e * T : (e + 1) * T],
                 in_=h_grouped[:, e].rearrange("p t k -> p (t k)"),
-            )
-
-        def store_h(k):
-            e, a = steps[k]
-            h_out = work.tile([P, P, J], F32, name="h_out")
-            nc.scalar.copy(out=h_out[:], in_=h_t[k][:].rearrange("t j p -> t p j"))
-            nc.sync.dma_start(
-                out=out_0[e][:, a * J * P : (a + 1) * J * P], in_=h_out[:].rearrange("t p j -> t (p j)")
             )
 
         a_grouped = keep.tile([P, E, R, PACK], BF16, align_bytes=64)
@@ -245,39 +312,10 @@ def tile_loralinearexpertswrapper_pa_s_kernel(tc, x, low_gu, W_gu, B_gu, A_d, ou
                 in_=a_grouped[:].rearrange("q e r k -> q (e r k)"),
             )
 
-        for b in range(-1, n_steps + 2):
-            if b + 1 < n_steps:
-                transpose_w(b + 1, GATE)
-                transpose_w(b + 1, UP)
-                regroup_w(b + 1, GATE)
-                regroup_w(b + 1, UP)
-            if b + 1 == n_steps:
-                transpose_a()
-            if 0 <= b < n_steps:
-                quantise_w(b, GATE)
-            if 0 <= b - 2 < n_steps:
-                round_h(b - 2)
-            if 0 <= b - 1 < n_steps:
-                add_lora(b - 1, GATE)
-                silu_gate(b - 1)
-            if 0 <= b - 2 < n_steps and steps[b - 2][1] == STEPS - 1:
-                quantise_h(steps[b - 2][0])
-            if 0 <= b - 1 < n_steps:
-                add_lora(b - 1, UP)
-            if 0 <= b < n_steps:
-                quantise_w(b, UP)
-                multiply(b)
-            if b == n_steps:
-                quantise_a()
-            if 0 <= b - 1 < n_steps:
-                product(b - 1)
-            if 0 <= b - 2 < n_steps:
-                store_h(b - 2)
-
-        low_d_ps = last.tile([P, E, R], F32, tag="last")
-        for e in range(E):
+        def project(e):
+            low_d_ps = flip.tile([P, R], F32, tag="flip", name="low_d_ps")
             nc.tensor.matmul_mx(
-                out=low_d_ps[:, e, :],
+                out=low_d_ps[:],
                 lhsT=h_codes[:, e * T : (e + 1) * T].bitcast(FP8X4),
                 lhsT_scale=h_scales[:, e * T : (e + 1) * T],
                 rhs=a_codes[:, e * R : (e + 1) * R].bitcast(FP8X4),
@@ -285,6 +323,75 @@ def tile_loralinearexpertswrapper_pa_s_kernel(tc, x, low_gu, W_gu, B_gu, A_d, ou
                 start=True,
                 stop=True,
             )
-        low_d_sb = keep.tile([P, E, R], F32)
-        nc.vector.tensor_copy(out=low_d_sb[:], in_=low_d_ps[:])
-        nc.sync.dma_start(out=out_1.rearrange("e t r -> t e r"), in_=low_d_sb[:])
+            low_d_sb = work.tile([P, R], F32, name="low_d_sb")
+            nc.vector.tensor_copy(out=low_d_sb[:], in_=low_d_ps[:])
+            nc.sync.dma_start(out=out_1[e], in_=low_d_sb[:])
+
+        substeps = [(k, j) for k in range(n_steps) for j in range(J)]
+        both = slice(0, J)
+
+        def w_in(m):
+            transpose_w(*substeps[m])
+
+        def w_out(m):
+            regroup_w(*substeps[m])
+
+        def w_mx(m):
+            quantise_w(*substeps[m])
+            multiply(*substeps[m])
+
+        transpose_low()
+        for a in range(STEPS):
+            transpose_b(0, a)
+            copy_b(0, a)
+        transpose_x()
+        for a in range(STEPS):
+            lora_term(0, a)
+        quantise_x()
+        for m in range(4):
+            w_in(m)
+            w_out(m)
+        for a in range(STEPS):
+            transpose_b(1, a)
+        w_mx(0)
+        w_mx(1)
+        for a in range(STEPS):
+            copy_b(1, a)
+        for k in range(n_steps - 1):
+            if k + 2 < n_steps:
+                for j in range(J):
+                    w_in(J * (k + 2) + j)
+                    w_out(J * (k + 2) + j)
+                lora_term(1, k)
+            else:
+                transpose_a()
+            w_mx(J * (k + 1))
+            add_lora(k, both)
+            silu_gate(k, both)
+            if k > 0:
+                product(k - 1)
+                store_h(k - 1)
+            w_mx(J * (k + 1) + 1)
+            if k > 0:
+                transpose_h(k - 1)
+            if k > 1:
+                round_h(k - 2)
+        k = n_steps - 1
+        add_lora(k, slice(0, 1))
+        silu_gate(k, slice(0, 1))
+        product(k - 1)
+        store_h(k - 1)
+        add_lora(k, slice(1, 2))
+        silu_gate(k, slice(1, 2))
+        round_h(k - 2)
+        quantise_a()
+        transpose_h(k - 1)
+        round_h(k - 1)
+        for j in range(J):
+            last_product(j)
+        last_round()
+        last_transpose()
+        quantise_h(0)
+        quantise_h(1)
+        project(0)
+        project(1)

@@ -19,9 +19,9 @@ PACK = 4
 PAIR = 2
 GATE, UP = 0, 1
 HALVES = 2
-STEPS = 2
-J = D // (STEPS * P)
-DS = J * P
+J = D // P
+JS = 2
+PIECES = J // JS
 WARM_PASSES = 3
 WARM_N = 256
 
@@ -30,8 +30,6 @@ FLOPS = 2 * E * T * (H * 2 * D + R * 2 * D + D * R)
 
 def tile_loralinearexpertswrapper_pa_s_kernel(tc, x, low_gu, W_gu, B_gu, A_d, out_0, out_1):
     nc = tc.nc
-    steps = [(e, a) for e in range(E) for a in range(STEPS)]
-    n_steps = len(steps)
     with ExitStack() as ctx:
         keep = ctx.enter_context(tc.tile_pool(name="keep", bufs=1))
         work = ctx.enter_context(tc.tile_pool(name="work", bufs=4))
@@ -41,34 +39,31 @@ def tile_loralinearexpertswrapper_pa_s_kernel(tc, x, low_gu, W_gu, B_gu, A_d, ou
 
         low_sb = keep.tile([P, E, R], BF16)
         nc.sync.dma_start(out=low_sb[:], in_=low_gu.rearrange("e t r -> t e r"))
-        b_rows = B_gu.rearrange("e (s a p j) r -> e a p s (j r)", s=HALVES, a=STEPS, p=P)
         b_sb = {}
-
-        def load_b(e, a):
-            b_sb[(e, a)] = keep.tile([P, HALVES, J * R], BF16, name="b_sb_%d_%d" % (e, a))
-            nc.sync.dma_start(out=b_sb[(e, a)][:], in_=b_rows[e, a])
-
-        x_sb = keep.tile([P, E, H], BF16)
-        a_sb = keep.tile([P, E, D], BF16)
-        w_rows = W_gu.rearrange("e (s a p j) h -> e a s p (j h)", s=HALVES, a=STEPS, p=P)
         w_sb = {}
 
-        def load_w(k):
-            e, a = steps[k]
-            for s in range(HALVES):
-                w_sb[(k, s)] = keep.tile([P, J * H], BF16, name="w_sb_%d_%d" % (k, s))
-                nc.sync.dma_start(out=w_sb[(k, s)][:], in_=w_rows[e, a, s])
+        def load_b(e):
+            b_sb[e] = keep.tile([P, HALVES, J * R], BF16, name="b_sb_%d" % e)
+            nc.sync.dma_start(out=b_sb[e][:], in_=B_gu.rearrange("e (s p j) r -> e p s (j r)", s=HALVES, p=P)[e])
 
-        load_b(0, 0)
-        load_b(0, 1)
-        nc.sync.dma_start(out=x_sb[:], in_=x.rearrange("e t h -> t e h"))
-        load_w(0)
-        load_w(1)
-        load_b(1, 0)
-        load_b(1, 1)
-        load_w(2)
+        def load_w(e, s):
+            w_sb[(e, s)] = keep.tile([P, J, H], BF16, name="w_sb_%d_%d" % (e, s))
+            nc.sync.dma_start(
+                out=w_sb[(e, s)][:], in_=W_gu.rearrange("e (s p j) h -> e s p j h", s=HALVES, p=P)[e, s]
+            )
+
+        load_b(0)
+        x_sb = keep.tile([P, PAIR, H], BF16)
+        nc.sync.dma_start(
+            out=x_sb[:], in_=x.rearrange("e t h -> (e t) h").rearrange("(p i) h -> p i h", i=PAIR)
+        )
+        load_w(0, GATE)
+        load_w(0, UP)
+        load_b(1)
+        load_w(1, GATE)
+        load_w(1, UP)
+        a_sb = keep.tile([P, E, D], BF16)
         nc.sync.dma_start(out=a_sb[:], in_=A_d.rearrange("e r d -> r e d"))
-        load_w(3)
 
         ident_bf16 = keep.tile([P, P], BF16)
         make_identity(nc, ident_bf16[:])
@@ -96,198 +91,206 @@ def tile_loralinearexpertswrapper_pa_s_kernel(tc, x, low_gu, W_gu, B_gu, A_d, ou
                 stop=True,
             )
 
-        def transpose_low():
-            low_t = flip.tile([P, E, T], BF16, tag="flip", name="low_t")
-            for e in range(E):
-                nc.tensor.transpose(low_t[:, e, :], low_sb[:, e, :], ident_bf16[:])
-            nc.scalar.copy(out=low_k[:], in_=low_t[:])
+        def copy_out(engine, out, in_):
+            if engine == "S":
+                nc.scalar.copy(out=out, in_=in_)
+            else:
+                nc.vector.tensor_copy(out=out, in_=in_)
+
+        psum = {}
 
         low_k = keep.tile([P, E, T], BF16)
-        b_k = keep.tile([P, E, STEPS, J * HALVES, P], BF16)
-        delta = keep.tile([P, E, STEPS, J, HALVES, P], F32)
-        b_t = {}
+        b_k = keep.tile([P, E, HALVES, J, P], BF16)
+        delta = keep.tile([P, E, HALVES, J * P], F32)
 
-        def transpose_b(e, a):
-            b_t[(e, a)] = flip.tile([P, J * HALVES, P], BF16, tag="flip", name="b_t")
+        def lowt():
+            psum["low"] = flip.tile([P, E, T], BF16, tag="flip", name="low_t")
+            for e in range(E):
+                nc.tensor.transpose(psum["low"][:, e, :], low_sb[:, e, :], ident_bf16[:])
+
+        def lowx():
+            nc.scalar.copy(out=low_k[:], in_=psum["low"][:])
+
+        def bt(e, s):
+            psum[("b", e, s)] = flip.tile([P, J, P], BF16, tag="flip", name="b_t")
             for j in range(J):
-                for s in range(HALVES):
-                    nc.tensor.transpose(
-                        b_t[(e, a)][:, j * HALVES + s, :], b_sb[(e, a)][:, s, j * R : (j + 1) * R], ident_bf16[:]
-                    )
+                nc.tensor.transpose(psum[("b", e, s)][:, j, :], b_sb[e][:, s, j * R : (j + 1) * R], ident_bf16[:])
 
-        def copy_b(e, a):
-            nc.vector.tensor_copy(out=b_k[:, e, a], in_=b_t[(e, a)][:])
+        def bx(e, s, engine):
+            copy_out(engine, b_k[:, e, s], psum[("b", e, s)][:])
 
-        def lora_term(e, a):
-            delta_ps = sums.tile([P, J * HALVES, P], F32, tag="sums", name="delta_ps")
-            if (e, a) == steps[-1]:
-                for c in range(J * HALVES):
-                    nc.tensor.matmul(
-                        delta_ps[:, c, :], lhsT=b_k[:, e, a, c, :], rhs=low_k[:, e, :], start=True, stop=True
-                    )
-            else:
+        def dm(e, s):
+            psum[("d", e, s)] = sums.tile([P, J * P], F32, tag="sums", name="delta_ps")
+            if e == 0:
                 nc.tensor.matmul(
-                    delta_ps[:].rearrange("t c p -> t (c p)"),
+                    psum[("d", e, s)][:],
                     lhsT=low_k[:, e, :],
-                    rhs=b_k[:, e, a].rearrange("r c p -> r (c p)"),
+                    rhs=b_k[:, e, s].rearrange("r j p -> r (j p)"),
                     start=True,
                     stop=True,
                 )
-            nc.scalar.copy(out=delta[:, e, a].rearrange("t j s p -> t (j s) p"), in_=delta_ps[:])
+            else:
+                for j in range(J):
+                    nc.tensor.matmul(
+                        psum[("d", e, s)][:, j * T : (j + 1) * T],
+                        lhsT=b_k[:, e, s, j, :],
+                        rhs=low_k[:, e, :],
+                        start=True,
+                        stop=True,
+                    )
 
-        def transpose_words(out, words):
-            for u in range(PAIR):
-                nc.tensor.transpose(out[:, u, :], words[:, u * P : (u + 1) * P], ident_f32[:])
+        def dx(e, s):
+            nc.scalar.copy(out=delta[:, e, s], in_=psum[("d", e, s)][:])
 
-        x_words = x_sb[:].bitcast(F32)
-        x_grouped = keep.tile([P, E, T, PACK], BF16, align_bytes=64)
+        def xt():
+            words = x_sb[:].bitcast(F32)
+            psum["x"] = flip.tile([P, PAIR, PAIR, P], F32, tag="flip", name="x_t")
+            for i in range(PAIR):
+                for u in range(PAIR):
+                    nc.tensor.transpose(psum["x"][:, i, u, :], words[:, i, u * P : (u + 1) * P], ident_f32[:])
+
+        x_grouped = keep.tile([P, P, PAIR, PACK], BF16, align_bytes=64)
         x_codes = keep.tile([P, E * T], U32, align_bytes=64)
         x_scales = keep.tile([P, E * T], U8, align_bytes=64)
 
-        def transpose_x():
-            x_t = flip.tile([P, E, PAIR, T], F32, tag="flip")
-            for e in range(E):
-                transpose_words(x_t[:, e], x_words[:, e, :])
-            nc.vector.tensor_copy(out=x_grouped[:].bitcast(F32), in_=x_t[:].rearrange("q e u t -> q e t u"))
+        def xx():
+            nc.vector.tensor_copy(out=x_grouped[:].bitcast(F32), in_=psum["x"][:].rearrange("q i u p -> q p i u"))
 
-        def quantise_x():
+        def xq():
             nc.vector.quantize_mx(
                 out=x_codes[:].bitcast(FP8X4),
                 scales=x_scales[:],
-                in_=x_grouped[:].rearrange("q e t k -> q (e t k)"),
+                in_=x_grouped[:].rearrange("q p i k -> q (p i k)"),
             )
 
-        w_t = {}
+        pieces = [(e, s, c) for e in range(E) for s in range(HALVES) for c in range(PIECES)]
         w_grouped = {}
         w_codes = {}
         w_scales = {}
-        base = {}
-        total = {}
-        gate_act = {}
-        h_f32 = {}
-        h_t = {}
-        h_grouped = keep.tile([P, E, T, PACK], BF16, align_bytes=64)
-        h_codes = keep.tile([P, E * T], U32, align_bytes=64)
-        h_scales = keep.tile([P, E * T], U8, align_bytes=64)
 
-        def transpose_w(k, j):
-            w_t[(k, j)] = flip.tile([P, HALVES, PAIR, P], F32, tag="flip", name="w_t")
-            for s in range(HALVES):
-                words = w_sb[(k, s)][:].bitcast(F32).rearrange("p (j w) -> p j w", j=J)
-                transpose_words(w_t[(k, j)][:, s], words[:, j, :])
+        def wt(m):
+            e, s, c = pieces[m]
+            words = w_sb[(e, s)][:].bitcast(F32)
+            psum[("w", m)] = flip.tile([P, JS, PAIR, P], F32, tag="flip", name="w_t")
+            for j in range(JS):
+                for u in range(PAIR):
+                    nc.tensor.transpose(
+                        psum[("w", m)][:, j, u, :], words[:, c * JS + j, u * P : (u + 1) * P], ident_f32[:]
+                    )
 
-        def regroup_w(k, j):
-            w_grouped[(k, j)] = work.tile([P, HALVES, P, PACK], BF16, align_bytes=64, name="w_grouped")
-            out = w_grouped[(k, j)][:].bitcast(F32)
-            in_ = w_t[(k, j)][:].rearrange("q s u p -> q s p u")
-            if (k, j) == (0, 1):
-                nc.vector.tensor_copy(out=out, in_=in_)
-            else:
-                nc.scalar.copy(out=out, in_=in_)
+        def wx(m, engine):
+            w_grouped[m] = work.tile([P, JS, P, PACK], BF16, align_bytes=64, name="w_grouped")
+            copy_out(engine, w_grouped[m][:].bitcast(F32), psum[("w", m)][:].rearrange("q j u p -> q j p u"))
 
-        def quantise_w(k, j):
-            w_codes[(k, j)] = work.tile([P, HALVES * P], U32, align_bytes=64, name="w_codes")
-            w_scales[(k, j)] = work.tile([P, HALVES * P], U8, align_bytes=64, name="w_scales")
+        def wq(m):
+            w_codes[m] = work.tile([P, JS * P], U32, align_bytes=64, name="w_codes")
+            w_scales[m] = work.tile([P, JS * P], U8, align_bytes=64, name="w_scales")
             nc.vector.quantize_mx(
-                out=w_codes[(k, j)][:].bitcast(FP8X4),
-                scales=w_scales[(k, j)][:],
-                in_=w_grouped[(k, j)][:].rearrange("q s p k -> q (s p k)"),
+                out=w_codes[m][:].bitcast(FP8X4),
+                scales=w_scales[m][:],
+                in_=w_grouped[m][:].rearrange("q j p k -> q (j p k)"),
             )
 
-        def multiply(k, j):
-            e = steps[k][0]
-            x_c, x_s = x_codes[:, e * T : (e + 1) * T], x_scales[:, e * T : (e + 1) * T]
-            w_c, w_s = w_codes[(k, j)], w_scales[(k, j)]
-            if j == 0 or k == n_steps - 1:
-                base[(k, j)] = sums.tile([P, J, HALVES, P], F32, tag="sums", name="base")
+        def mm(m):
+            e, s, c = pieces[m]
+            if c == 0:
+                psum[("base", e, s)] = sums.tile([P, J * P], F32, tag="sums", name="base")
+            out = psum[("base", e, s)][:, c * JS * P : (c + 1) * JS * P]
+            x_c, x_s = x_codes[:, e * T : (e + 1) * T].bitcast(FP8X4), x_scales[:, e * T : (e + 1) * T]
+            if e == 0:
+                nc.tensor.matmul_mx(
+                    out=out,
+                    lhsT=x_c,
+                    lhsT_scale=x_s,
+                    rhs=w_codes[m][:].bitcast(FP8X4),
+                    rhs_scale=w_scales[m][:],
+                    start=True,
+                    stop=True,
+                )
             else:
-                base[(k, j)] = base[(k, 0)]
-            if k == n_steps - 1:
-                for s in range(HALVES):
+                for j in range(JS):
+                    one = slice(j * P, (j + 1) * P)
                     nc.tensor.matmul_mx(
-                        out=base[(k, j)][:, j, s, :],
-                        lhsT=w_c[:, s * P : (s + 1) * P].bitcast(FP8X4),
-                        lhsT_scale=w_s[:, s * P : (s + 1) * P],
-                        rhs=x_c.bitcast(FP8X4),
+                        out=out[:, one],
+                        lhsT=w_codes[m][:, one].bitcast(FP8X4),
+                        lhsT_scale=w_scales[m][:, one],
+                        rhs=x_c,
                         rhs_scale=x_s,
                         start=True,
                         stop=True,
                     )
-            else:
-                nc.tensor.matmul_mx(
-                    out=base[(k, j)][:, j].rearrange("t s p -> t (s p)"),
-                    lhsT=x_c.bitcast(FP8X4),
-                    lhsT_scale=x_s,
-                    rhs=w_c[:].bitcast(FP8X4),
-                    rhs_scale=w_s[:],
-                    start=True,
-                    stop=True,
-                )
 
-        def add_lora(k, js):
-            e, a = steps[k]
-            if js.start == 0:
-                total[k] = work.tile([P, J, HALVES, P], F32, name="total")
+        total = {(e, s): keep.tile([P, J * P], F32, name="total_%d_%d" % (e, s)) for e in range(E) for s in range(HALVES)}
+        gate_act = {e: keep.tile([P, J * P], F32, name="gate_act_%d" % e) for e in range(E)}
+        whole = slice(0, J * P)
+        piece = [slice(c * JS * P, (c + 1) * JS * P) for c in range(PIECES)]
+
+        def add(e, s, cols):
             nc.vector.scalar_tensor_tensor(
-                out=total[k][:, js],
-                in0=delta[:, e, a, js],
+                out=total[(e, s)][:, cols],
+                in0=delta[:, e, s, cols],
                 scalar=LORA_SCALE,
-                in1=base[(k, js.start)][:, js],
+                in1=psum[("base", e, s)][:, cols],
                 op0=ALU.mult,
                 op1=ALU.add,
             )
 
-        def silu_gate(k, js):
-            if js.start == 0:
-                gate_act[k] = work.tile([P, J, P], F32, name="gate_act")
-            nc.scalar.activation(out=gate_act[k][:, js], in_=total[k][:, js, GATE], func=ACT.Silu)
+        def silu(e):
+            nc.scalar.activation(out=gate_act[e][:], in_=total[(e, GATE)][:], func=ACT.Silu)
 
-        def product(k):
-            h_f32[k] = work.tile([P, P, J], F32, name="h_f32")
-            nc.vector.tensor_tensor(
-                out=h_f32[k][:],
-                in0=total[k][:, :, UP].rearrange("t j p -> t p j"),
-                in1=gate_act[k][:].rearrange("t j p -> t p j"),
+        h_grouped = keep.tile([P, E, T, PACK], BF16, align_bytes=64)
+        h_codes = keep.tile([P, E * T], U32, align_bytes=64)
+        h_scales = keep.tile([P, E * T], U8, align_bytes=64)
+        h0 = keep.tile([P, P, J], F32)
+        h1 = keep.tile([P, J * P], F32)
+        h1_out = keep.tile([P, P, J], F32)
+
+        def pr0():
+            nc.gpsimd.tensor_tensor(
+                out=h0[:],
+                in0=total[(0, UP)][:].rearrange("t (j p) -> t p j", j=J),
+                in1=gate_act[0][:].rearrange("t (j p) -> t p j", j=J),
                 op=ALU.mult,
             )
+            nc.sync.dma_start(out=out_0[0], in_=h0[:].rearrange("t p j -> t (p j)"))
 
-        def store_h(k):
-            e, a = steps[k]
-            nc.sync.dma_start(out=out_0[e][:, a * DS : (a + 1) * DS], in_=h_f32[k][:].rearrange("t p j -> t (p j)"))
+        def ht0():
+            h = h0[:].rearrange("t p j -> t (p j)")
+            psum["h0"] = flip.tile([P, PAIR, PAIR, T], F32, tag="flip", name="h0_t")
+            for u in range(PAIR):
+                for i in range(PAIR):
+                    nc.tensor.transpose(
+                        psum["h0"][:, u, i, :], h[:, u * PAIR * P + i : (u + 1) * PAIR * P : PAIR], ident_f32[:]
+                    )
 
-        def transpose_h(k):
-            h_t[k] = flip.tile([P, J, T], F32, tag="flip", name="h_t")
-            for j in range(J):
-                nc.tensor.transpose(h_t[k][:, j, :], h_f32[k][:, :, j], ident_f32[:])
+        def hx0():
+            nc.scalar.copy(
+                out=h_grouped[:, 0].rearrange("q t (u i) -> q t u i", u=PAIR),
+                in_=psum["h0"][:].rearrange("q u i t -> q t u i"),
+            )
 
-        def round_h(k):
-            e, a = steps[k]
-            nc.scalar.copy(out=h_grouped[:, e, :, a * J : (a + 1) * J], in_=h_t[k][:].rearrange("p j t -> p t j"))
-
-        h_turned = keep.tile([P, J, T], F32)
-
-        def last_product(j):
-            k = n_steps - 1
+        def pr1(c):
             nc.vector.tensor_tensor(
-                out=h_turned[:, j], in0=total[k][:, j, UP], in1=gate_act[k][:, j], op=ALU.mult
+                out=h1[:, piece[c]], in0=total[(1, UP)][:, piece[c]], in1=gate_act[1][:, piece[c]], op=ALU.mult
             )
 
-        def last_round():
-            e, a = steps[-1]
-            nc.vector.tensor_copy(
-                out=h_grouped[:, e, :, a * J : (a + 1) * J], in_=h_turned[:].rearrange("p j t -> p t j")
+        def ro1():
+            nc.vector.tensor_copy(out=h_grouped[:, 1], in_=h1[:].rearrange("p (j t) -> p t j", j=J))
+
+        def ht1(c):
+            if c == 0:
+                psum["h1"] = flip.tile([P, J, P], F32, tag="flip", name="h1_t")
+            for j in range(c * JS, (c + 1) * JS):
+                nc.tensor.transpose(psum["h1"][:, j, :], h1[:, j * T : (j + 1) * T], ident_f32[:])
+
+        def so(half):
+            ps = slice(half * P // 2, (half + 1) * P // 2)
+            nc.scalar.copy(out=h1_out[:, ps], in_=psum["h1"][:].rearrange("t j p -> t p j")[:, ps])
+            nc.sync.dma_start(
+                out=out_0[1][:, half * D // 2 : (half + 1) * D // 2], in_=h1_out[:, ps].rearrange("t p j -> t (p j)")
             )
 
-        def last_transpose():
-            k = n_steps - 1
-            h_t[k] = flip.tile([P, J, P], F32, tag="flip", name="h_t")
-            for j in range(J):
-                nc.tensor.transpose(h_t[k][:, j, :], h_turned[:, j], ident_f32[:])
-            h_f32[k] = work.tile([P, P, J], F32, name="h_f32")
-            nc.scalar.copy(out=h_f32[k][:], in_=h_t[k][:].rearrange("t j p -> t p j"))
-            store_h(k)
-
-        def quantise_h(e):
+        def hq(e):
             nc.vector.quantize_mx(
                 out=h_codes[:, e * T : (e + 1) * T].bitcast(FP8X4),
                 scales=h_scales[:, e * T : (e + 1) * T],
@@ -298,24 +301,28 @@ def tile_loralinearexpertswrapper_pa_s_kernel(tc, x, low_gu, W_gu, B_gu, A_d, ou
         a_codes = keep.tile([P, E * R], U32, align_bytes=64)
         a_scales = keep.tile([P, E * R], U8, align_bytes=64)
 
-        def transpose_a():
-            a_words = a_sb[:].bitcast(F32)
-            a_t = flip.tile([P, E, PAIR, R], F32, tag="flip")
-            for e in range(E):
-                transpose_words(a_t[:, e], a_words[:, e, :])
-            nc.scalar.copy(out=a_grouped[:].bitcast(F32), in_=a_t[:].rearrange("q e u r -> q e r u"))
+        def at():
+            words = a_sb[:].bitcast(F32)
+            psum["a"] = flip.tile([P, E, PAIR, R], F32, tag="flip", name="a_t")
+            for u in range(PAIR):
+                nc.tensor.transpose(psum["a"][:, 0, u, :], words[:, 0, u * P : (u + 1) * P], ident_f32[:])
+            for u in range(PAIR):
+                nc.tensor.transpose(psum["a"][:, 1, u, :], words[:, 1, u::PAIR], ident_f32[:])
 
-        def quantise_a():
+        def ax():
+            nc.scalar.copy(out=a_grouped[:].bitcast(F32), in_=psum["a"][:].rearrange("q e u r -> q e r u"))
+
+        def aq():
             nc.vector.quantize_mx(
                 out=a_codes[:].bitcast(FP8X4),
                 scales=a_scales[:],
                 in_=a_grouped[:].rearrange("q e r k -> q (e r k)"),
             )
 
-        def project(e):
-            low_d_ps = flip.tile([P, R], F32, tag="flip", name="low_d_ps")
+        def lm(e):
+            psum[("low_d", e)] = flip.tile([P, R], F32, tag="flip", name="low_d_ps")
             nc.tensor.matmul_mx(
-                out=low_d_ps[:],
+                out=psum[("low_d", e)][:],
                 lhsT=h_codes[:, e * T : (e + 1) * T].bitcast(FP8X4),
                 lhsT_scale=h_scales[:, e * T : (e + 1) * T],
                 rhs=a_codes[:, e * R : (e + 1) * R].bitcast(FP8X4),
@@ -323,75 +330,85 @@ def tile_loralinearexpertswrapper_pa_s_kernel(tc, x, low_gu, W_gu, B_gu, A_d, ou
                 start=True,
                 stop=True,
             )
+
+        def lx(e, engine):
             low_d_sb = work.tile([P, R], F32, name="low_d_sb")
-            nc.vector.tensor_copy(out=low_d_sb[:], in_=low_d_ps[:])
+            copy_out(engine, low_d_sb[:], psum[("low_d", e)][:])
             nc.sync.dma_start(out=out_1[e], in_=low_d_sb[:])
 
-        substeps = [(k, j) for k in range(n_steps) for j in range(J)]
-        both = slice(0, J)
-
-        def w_in(m):
-            transpose_w(*substeps[m])
-
-        def w_out(m):
-            regroup_w(*substeps[m])
-
-        def w_mx(m):
-            quantise_w(*substeps[m])
-            multiply(*substeps[m])
-
-        transpose_low()
-        for a in range(STEPS):
-            transpose_b(0, a)
-            copy_b(0, a)
-        transpose_x()
-        for a in range(STEPS):
-            lora_term(0, a)
-        quantise_x()
+        lowt()
+        lowx()
+        bt(0, GATE)
+        bx(0, GATE, "V")
+        xt()
+        xx()
+        bt(0, UP)
+        bx(0, UP, "V")
+        dm(0, GATE)
+        dx(0, GATE)
+        xq()
+        wt(0)
+        wx(0, "V")
+        wt(1)
+        wx(1, "S")
+        dm(0, UP)
+        dx(0, UP)
+        wt(2)
+        wx(2, "S")
+        wt(3)
+        bt(1, GATE)
+        bt(1, UP)
+        wq(0)
+        wq(1)
+        wx(3, "V")
+        bx(1, GATE, "S")
+        bx(1, UP, "S")
+        wt(4)
+        wx(4, "S")
+        wt(5)
+        dm(1, GATE)
+        dx(1, GATE)
+        wq(2)
+        wx(5, "V")
+        wt(6)
+        wx(6, "S")
+        wq(3)
+        wq(4)
+        wq(5)
         for m in range(4):
-            w_in(m)
-            w_out(m)
-        for a in range(STEPS):
-            transpose_b(1, a)
-        w_mx(0)
-        w_mx(1)
-        for a in range(STEPS):
-            copy_b(1, a)
-        for k in range(n_steps - 1):
-            if k + 2 < n_steps:
-                for j in range(J):
-                    w_in(J * (k + 2) + j)
-                    w_out(J * (k + 2) + j)
-                lora_term(1, k)
-            else:
-                transpose_a()
-            w_mx(J * (k + 1))
-            add_lora(k, both)
-            silu_gate(k, both)
-            if k > 0:
-                product(k - 1)
-                store_h(k - 1)
-            w_mx(J * (k + 1) + 1)
-            if k > 0:
-                transpose_h(k - 1)
-            if k > 1:
-                round_h(k - 2)
-        k = n_steps - 1
-        add_lora(k, slice(0, 1))
-        silu_gate(k, slice(0, 1))
-        product(k - 1)
-        store_h(k - 1)
-        add_lora(k, slice(1, 2))
-        silu_gate(k, slice(1, 2))
-        round_h(k - 2)
-        quantise_a()
-        transpose_h(k - 1)
-        round_h(k - 1)
-        for j in range(J):
-            last_product(j)
-        last_round()
-        last_transpose()
-        quantise_h(0)
-        quantise_h(1)
-        project(0)
-        project(1)
+            mm(m)
+        wt(7)
+        wx(7, "S")
+        add(0, GATE, whole)
+        silu(0)
+        add(0, UP, whole)
+        mm(4)
+        mm(5)
+        wq(6)
+        dm(1, UP)
+        dx(1, UP)
+        at()
+        add(1, GATE, whole)
+        silu(1)
+        mm(6)
+        wq(7)
+        mm(7)
+        pr0()
+        ax()
+        ht0()
+        hx0()
+        for c in range(PIECES):
+            add(1, UP, piece[c])
+        for c in range(PIECES):
+            pr1(c)
+            ht1(c)
+        aq()
+        ro1()
+        so(0)
+        so(1)
+        hq(0)
+        lm(0)
+        hq(1)
+        lm(1)
+        lx(0, "S")
+        lx(1, "V")

@@ -66,9 +66,10 @@ def tile_loralinearexpertswrapper_pa_s_kernel(tc, x, low_gu, W_gu, B_gu, A_d, ou
         nc.sync.dma_start(out=a_sb[:], in_=A_d.rearrange("e r d -> r e d"))
 
         ident_bf16 = keep.tile([P, P], BF16)
-        make_identity(nc, ident_bf16[:])
         ident_f32 = keep.tile([P, P], F32)
-        make_identity(nc, ident_f32[:])
+        for ident in (ident_bf16, ident_f32):
+            nc.vector.memset(ident[:], 0.0)
+            make_identity(nc, ident[:], nomemset=True)
         zero = keep.tile([P, 1], F32)
         nc.vector.memset(zero[:], 0.0)
         unused = keep.tile([P, 1], F32)
@@ -111,13 +112,14 @@ def tile_loralinearexpertswrapper_pa_s_kernel(tc, x, low_gu, W_gu, B_gu, A_d, ou
         def lowx():
             nc.scalar.copy(out=low_k[:], in_=psum["low"][:])
 
-        def bt(e, s):
-            psum[("b", e, s)] = flip.tile([P, J, P], BF16, tag="flip", name="b_t")
-            for j in range(J):
-                nc.tensor.transpose(psum[("b", e, s)][:, j, :], b_sb[e][:, s, j * R : (j + 1) * R], ident_bf16[:])
+        def bt(e):
+            psum[("b", e)] = flip.tile([P, HALVES, J, P], BF16, tag="flip", name="b_t")
+            for s in range(HALVES):
+                for j in range(J):
+                    nc.tensor.transpose(psum[("b", e)][:, s, j, :], b_sb[e][:, s, j * R : (j + 1) * R], ident_bf16[:])
 
-        def bx(e, s, engine):
-            copy_out(engine, b_k[:, e, s], psum[("b", e, s)][:])
+        def bx(e, engine):
+            copy_out(engine, b_k[:, e], psum[("b", e)][:])
 
         def dm(e, s):
             psum[("d", e, s)] = sums.tile([P, J * P], F32, tag="sums", name="delta_ps")
@@ -163,57 +165,63 @@ def tile_loralinearexpertswrapper_pa_s_kernel(tc, x, low_gu, W_gu, B_gu, A_d, ou
                 in_=x_grouped[:].rearrange("q p i k -> q (p i k)"),
             )
 
-        pieces = [(e, s, c) for e in range(E) for s in range(HALVES) for c in range(PIECES)]
+        halves = [(e, s) for e in range(E) for s in range(HALVES)]
         w_grouped = {}
         w_codes = {}
         w_scales = {}
 
         def wt(m):
-            e, s, c = pieces[m]
-            words = w_sb[(e, s)][:].bitcast(F32)
+            words = w_sb[halves[m // PIECES]][:].bitcast(F32)
             psum[("w", m)] = flip.tile([P, JS, PAIR, P], F32, tag="flip", name="w_t")
             for j in range(JS):
                 for u in range(PAIR):
                     nc.tensor.transpose(
-                        psum[("w", m)][:, j, u, :], words[:, c * JS + j, u * P : (u + 1) * P], ident_f32[:]
+                        psum[("w", m)][:, j, u, :],
+                        words[:, m % PIECES * JS + j, u * P : (u + 1) * P],
+                        ident_f32[:],
                     )
 
         def wx(m, engine):
-            w_grouped[m] = work.tile([P, JS, P, PACK], BF16, align_bytes=64, name="w_grouped")
-            copy_out(engine, w_grouped[m][:].bitcast(F32), psum[("w", m)][:].rearrange("q j u p -> q j p u"))
-
-        def wq(m):
-            w_codes[m] = work.tile([P, JS * P], U32, align_bytes=64, name="w_codes")
-            w_scales[m] = work.tile([P, JS * P], U8, align_bytes=64, name="w_scales")
-            nc.vector.quantize_mx(
-                out=w_codes[m][:].bitcast(FP8X4),
-                scales=w_scales[m][:],
-                in_=w_grouped[m][:].rearrange("q j p k -> q (j p k)"),
+            n, c = m // PIECES, m % PIECES
+            if n not in w_grouped:
+                w_grouped[n] = work.tile([P, J, P, PACK], BF16, align_bytes=64, name="w_grouped")
+            copy_out(
+                engine,
+                w_grouped[n][:, c * JS : (c + 1) * JS].bitcast(F32),
+                psum[("w", m)][:].rearrange("q j u p -> q j p u"),
             )
 
-        def mm(m):
-            e, s, c = pieces[m]
-            if c == 0:
-                psum[("base", e, s)] = sums.tile([P, J * P], F32, tag="sums", name="base")
-            out = psum[("base", e, s)][:, c * JS * P : (c + 1) * JS * P]
+        def wq(n):
+            w_codes[n] = work.tile([P, J * P], U32, align_bytes=64, name="w_codes")
+            w_scales[n] = work.tile([P, J * P], U8, align_bytes=64, name="w_scales")
+            nc.vector.quantize_mx(
+                out=w_codes[n][:].bitcast(FP8X4),
+                scales=w_scales[n][:],
+                in_=w_grouped[n][:].rearrange("q j p k -> q (j p k)"),
+            )
+
+        def mm(n):
+            e, s = halves[n]
+            psum[("base", e, s)] = sums.tile([P, J * P], F32, tag="sums", name="base")
+            out = psum[("base", e, s)]
             x_c, x_s = x_codes[:, e * T : (e + 1) * T].bitcast(FP8X4), x_scales[:, e * T : (e + 1) * T]
             if e == 0:
                 nc.tensor.matmul_mx(
-                    out=out,
+                    out=out[:],
                     lhsT=x_c,
                     lhsT_scale=x_s,
-                    rhs=w_codes[m][:].bitcast(FP8X4),
-                    rhs_scale=w_scales[m][:],
+                    rhs=w_codes[n][:].bitcast(FP8X4),
+                    rhs_scale=w_scales[n][:],
                     start=True,
                     stop=True,
                 )
             else:
-                for j in range(JS):
+                for j in range(J):
                     one = slice(j * P, (j + 1) * P)
                     nc.tensor.matmul_mx(
                         out=out[:, one],
-                        lhsT=w_codes[m][:, one].bitcast(FP8X4),
-                        lhsT_scale=w_scales[m][:, one],
+                        lhsT=w_codes[n][:, one].bitcast(FP8X4),
+                        lhsT_scale=w_scales[n][:, one],
                         rhs=x_c,
                         rhs_scale=x_s,
                         start=True,
@@ -222,15 +230,12 @@ def tile_loralinearexpertswrapper_pa_s_kernel(tc, x, low_gu, W_gu, B_gu, A_d, ou
 
         total = {(e, s): keep.tile([P, J * P], F32, name="total_%d_%d" % (e, s)) for e in range(E) for s in range(HALVES)}
         gate_act = {e: keep.tile([P, J * P], F32, name="gate_act_%d" % e) for e in range(E)}
-        whole = slice(0, J * P)
-        piece = [slice(c * JS * P, (c + 1) * JS * P) for c in range(PIECES)]
-
-        def add(e, s, cols):
+        def add(e, s):
             nc.vector.scalar_tensor_tensor(
-                out=total[(e, s)][:, cols],
-                in0=delta[:, e, s, cols],
+                out=total[(e, s)][:],
+                in0=delta[:, e, s],
                 scalar=LORA_SCALE,
-                in1=psum[("base", e, s)][:, cols],
+                in1=psum[("base", e, s)][:],
                 op0=ALU.mult,
                 op1=ALU.add,
             )
@@ -246,7 +251,7 @@ def tile_loralinearexpertswrapper_pa_s_kernel(tc, x, low_gu, W_gu, B_gu, A_d, ou
         h1_out = keep.tile([P, P, J], F32)
 
         def pr0():
-            nc.gpsimd.tensor_tensor(
+            nc.vector.tensor_tensor(
                 out=h0[:],
                 in0=total[(0, UP)][:].rearrange("t (j p) -> t p j", j=J),
                 in1=gate_act[0][:].rearrange("t (j p) -> t p j", j=J),
@@ -269,18 +274,15 @@ def tile_loralinearexpertswrapper_pa_s_kernel(tc, x, low_gu, W_gu, B_gu, A_d, ou
                 in_=psum["h0"][:].rearrange("q u i t -> q t u i"),
             )
 
-        def pr1(c):
-            nc.vector.tensor_tensor(
-                out=h1[:, piece[c]], in0=total[(1, UP)][:, piece[c]], in1=gate_act[1][:, piece[c]], op=ALU.mult
-            )
+        def pr1():
+            nc.vector.tensor_tensor(out=h1[:], in0=total[(1, UP)][:], in1=gate_act[1][:], op=ALU.mult)
 
         def ro1():
             nc.vector.tensor_copy(out=h_grouped[:, 1], in_=h1[:].rearrange("p (j t) -> p t j", j=J))
 
-        def ht1(c):
-            if c == 0:
-                psum["h1"] = flip.tile([P, J, P], F32, tag="flip", name="h1_t")
-            for j in range(c * JS, (c + 1) * JS):
+        def ht1():
+            psum["h1"] = flip.tile([P, J, P], F32, tag="flip", name="h1_t")
+            for j in range(J):
                 nc.tensor.transpose(psum["h1"][:, j, :], h1[:, j * T : (j + 1) * T], ident_f32[:])
 
         def so(half):
@@ -290,11 +292,11 @@ def tile_loralinearexpertswrapper_pa_s_kernel(tc, x, low_gu, W_gu, B_gu, A_d, ou
                 out=out_0[1][:, half * D // 2 : (half + 1) * D // 2], in_=h1_out[:, ps].rearrange("t p j -> t (p j)")
             )
 
-        def hq(e):
+        def hq():
             nc.vector.quantize_mx(
-                out=h_codes[:, e * T : (e + 1) * T].bitcast(FP8X4),
-                scales=h_scales[:, e * T : (e + 1) * T],
-                in_=h_grouped[:, e].rearrange("p t k -> p (t k)"),
+                out=h_codes[:].bitcast(FP8X4),
+                scales=h_scales[:],
+                in_=h_grouped[:].rearrange("p e t k -> p (e t k)"),
             )
 
         a_grouped = keep.tile([P, E, R, PACK], BF16, align_bytes=64)
@@ -319,96 +321,82 @@ def tile_loralinearexpertswrapper_pa_s_kernel(tc, x, low_gu, W_gu, B_gu, A_d, ou
                 in_=a_grouped[:].rearrange("q e r k -> q (e r k)"),
             )
 
-        def lm(e):
-            psum[("low_d", e)] = flip.tile([P, R], F32, tag="flip", name="low_d_ps")
-            nc.tensor.matmul_mx(
-                out=psum[("low_d", e)][:],
-                lhsT=h_codes[:, e * T : (e + 1) * T].bitcast(FP8X4),
-                lhsT_scale=h_scales[:, e * T : (e + 1) * T],
-                rhs=a_codes[:, e * R : (e + 1) * R].bitcast(FP8X4),
-                rhs_scale=a_scales[:, e * R : (e + 1) * R],
-                start=True,
-                stop=True,
-            )
+        def lm():
+            psum["low_d"] = flip.tile([P, E, R], F32, tag="flip", name="low_d_ps")
+            for e in range(E):
+                nc.tensor.matmul_mx(
+                    out=psum["low_d"][:, e, :],
+                    lhsT=h_codes[:, e * T : (e + 1) * T].bitcast(FP8X4),
+                    lhsT_scale=h_scales[:, e * T : (e + 1) * T],
+                    rhs=a_codes[:, e * R : (e + 1) * R].bitcast(FP8X4),
+                    rhs_scale=a_scales[:, e * R : (e + 1) * R],
+                    start=True,
+                    stop=True,
+                )
 
-        def lx(e, engine):
-            low_d_sb = work.tile([P, R], F32, name="low_d_sb")
-            copy_out(engine, low_d_sb[:], psum[("low_d", e)][:])
-            nc.sync.dma_start(out=out_1[e], in_=low_d_sb[:])
+        def lx():
+            low_d_sb = keep.tile([P, E, R], F32)
+            nc.scalar.copy(out=low_d_sb[:], in_=psum["low_d"][:])
+            nc.sync.dma_start(out=out_1.rearrange("e t r -> t e r"), in_=low_d_sb[:])
 
         lowt()
         lowx()
-        bt(0, GATE)
-        bx(0, GATE, "V")
+        bt(0)
+        bx(0, "V")
         xt()
         xx()
-        bt(0, UP)
-        bx(0, UP, "V")
+        wt(0)
+        wx(0, "S")
+        wt(1)
+        wx(1, "V")
+        xq()
         dm(0, GATE)
         dx(0, GATE)
-        xq()
-        wt(0)
-        wx(0, "V")
-        wt(1)
-        wx(1, "S")
-        dm(0, UP)
-        dx(0, UP)
         wt(2)
         wx(2, "S")
-        wt(3)
-        bt(1, GATE)
-        bt(1, UP)
         wq(0)
-        wq(1)
+        wt(3)
         wx(3, "V")
-        bx(1, GATE, "S")
-        bx(1, UP, "S")
+        dm(0, UP)
+        dx(0, UP)
+        bt(1)
+        bx(1, "S")
+        wq(1)
         wt(4)
         wx(4, "S")
         wt(5)
-        dm(1, GATE)
-        dx(1, GATE)
-        wq(2)
         wx(5, "V")
+        mm(0)
+        add(0, GATE)
         wt(6)
         wx(6, "S")
-        wq(3)
-        wq(4)
-        wq(5)
-        for m in range(4):
-            mm(m)
+        wq(2)
         wt(7)
         wx(7, "S")
-        add(0, GATE, whole)
+        mm(1)
+        add(0, UP)
+        dm(1, GATE)
+        dx(1, GATE)
         silu(0)
-        add(0, UP, whole)
-        mm(4)
-        mm(5)
-        wq(6)
         dm(1, UP)
         dx(1, UP)
+        wq(3)
+        mm(2)
         at()
-        add(1, GATE, whole)
-        silu(1)
-        mm(6)
-        wq(7)
-        mm(7)
-        pr0()
         ax()
+        mm(3)
+        add(1, GATE)
+        silu(1)
+        pr0()
         ht0()
         hx0()
-        for c in range(PIECES):
-            add(1, UP, piece[c])
-        for c in range(PIECES):
-            pr1(c)
-            ht1(c)
+        add(1, UP)
         aq()
-        ro1()
+        pr1()
+        ht1()
         so(0)
         so(1)
-        hq(0)
-        lm(0)
-        hq(1)
-        lm(1)
-        lx(0, "S")
-        lx(1, "V")
+        ro1()
+        hq()
+        lm()
+        lx()

@@ -100,6 +100,12 @@ def tile_loralinearexpertswrapper_pa_s_kernel(tc, x, low_gu, W_gu, B_gu, A_d, ou
 
         psum = {}
 
+        def from_psum(e, ap):
+            return ap.rearrange("t (j p) -> t p j", j=J) if e == 0 else ap
+
+        def by_d(e, ap):
+            return ap.rearrange("t (p j) -> t p j", j=J) if e == 0 else ap
+
         low_k = keep.tile([P, E, T], BF16)
         b_k = keep.tile([P, E, HALVES, J, P], BF16)
         delta = keep.tile([P, E, HALVES, J * P], F32)
@@ -112,14 +118,16 @@ def tile_loralinearexpertswrapper_pa_s_kernel(tc, x, low_gu, W_gu, B_gu, A_d, ou
         def lowx():
             nc.scalar.copy(out=low_k[:], in_=psum["low"][:])
 
-        def bt(e):
-            psum[("b", e)] = flip.tile([P, HALVES, J, P], BF16, tag="flip", name="b_t")
-            for s in range(HALVES):
+        def bt(e, ss):
+            psum[("b", e, ss[0])] = flip.tile([P, len(ss), J, P], BF16, tag="flip", name="b_t")
+            for s in ss:
                 for j in range(J):
-                    nc.tensor.transpose(psum[("b", e)][:, s, j, :], b_sb[e][:, s, j * R : (j + 1) * R], ident_bf16[:])
+                    nc.tensor.transpose(
+                        psum[("b", e, ss[0])][:, s - ss[0], j, :], b_sb[e][:, s, j * R : (j + 1) * R], ident_bf16[:]
+                    )
 
-        def bx(e, engine):
-            copy_out(engine, b_k[:, e], psum[("b", e)][:])
+        def bx(e, ss, engine):
+            copy_out(engine, b_k[:, e, ss[0] : ss[-1] + 1], psum[("b", e, ss[0])][:])
 
         def dm(e, s):
             psum[("d", e, s)] = sums.tile([P, J * P], F32, tag="sums", name="delta_ps")
@@ -142,7 +150,7 @@ def tile_loralinearexpertswrapper_pa_s_kernel(tc, x, low_gu, W_gu, B_gu, A_d, ou
                     )
 
         def dx(e, s):
-            nc.scalar.copy(out=delta[:, e, s], in_=psum[("d", e, s)][:])
+            nc.scalar.copy(out=by_d(e, delta[:, e, s]), in_=from_psum(e, psum[("d", e, s)][:]))
 
         def xt():
             words = x_sb[:].bitcast(F32)
@@ -232,10 +240,10 @@ def tile_loralinearexpertswrapper_pa_s_kernel(tc, x, low_gu, W_gu, B_gu, A_d, ou
         gate_act = {e: keep.tile([P, J * P], F32, name="gate_act_%d" % e) for e in range(E)}
         def add(e, s):
             nc.vector.scalar_tensor_tensor(
-                out=total[(e, s)][:],
-                in0=delta[:, e, s],
+                out=by_d(e, total[(e, s)][:]),
+                in0=by_d(e, delta[:, e, s]),
                 scalar=LORA_SCALE,
-                in1=psum[("base", e, s)][:],
+                in1=from_psum(e, psum[("base", e, s)][:]),
                 op0=ALU.mult,
                 op1=ALU.add,
             )
@@ -246,26 +254,20 @@ def tile_loralinearexpertswrapper_pa_s_kernel(tc, x, low_gu, W_gu, B_gu, A_d, ou
         h_grouped = keep.tile([P, E, T, PACK], BF16, align_bytes=64)
         h_codes = keep.tile([P, E * T], U32, align_bytes=64)
         h_scales = keep.tile([P, E * T], U8, align_bytes=64)
-        h0 = keep.tile([P, P, J], F32)
+        h0 = keep.tile([P, D], F32)
         h1 = keep.tile([P, J * P], F32)
         h1_out = keep.tile([P, P, J], F32)
 
         def pr0():
-            nc.vector.tensor_tensor(
-                out=h0[:],
-                in0=total[(0, UP)][:].rearrange("t (j p) -> t p j", j=J),
-                in1=gate_act[0][:].rearrange("t (j p) -> t p j", j=J),
-                op=ALU.mult,
-            )
-            nc.sync.dma_start(out=out_0[0], in_=h0[:].rearrange("t p j -> t (p j)"))
+            nc.vector.tensor_tensor(out=h0[:], in0=total[(0, UP)][:], in1=gate_act[0][:], op=ALU.mult)
+            nc.sync.dma_start(out=out_0[0], in_=h0[:])
 
         def ht0():
-            h = h0[:].rearrange("t p j -> t (p j)")
             psum["h0"] = flip.tile([P, PAIR, PAIR, T], F32, tag="flip", name="h0_t")
             for u in range(PAIR):
                 for i in range(PAIR):
                     nc.tensor.transpose(
-                        psum["h0"][:, u, i, :], h[:, u * PAIR * P + i : (u + 1) * PAIR * P : PAIR], ident_f32[:]
+                        psum["h0"][:, u, i, :], h0[:, u * PAIR * P + i : (u + 1) * PAIR * P : PAIR], ident_f32[:]
                     )
 
         def hx0():
@@ -285,18 +287,15 @@ def tile_loralinearexpertswrapper_pa_s_kernel(tc, x, low_gu, W_gu, B_gu, A_d, ou
             for j in range(J):
                 nc.tensor.transpose(psum["h1"][:, j, :], h1[:, j * T : (j + 1) * T], ident_f32[:])
 
-        def so(half):
-            ps = slice(half * P // 2, (half + 1) * P // 2)
-            nc.scalar.copy(out=h1_out[:, ps], in_=psum["h1"][:].rearrange("t j p -> t p j")[:, ps])
-            nc.sync.dma_start(
-                out=out_0[1][:, half * D // 2 : (half + 1) * D // 2], in_=h1_out[:, ps].rearrange("t p j -> t (p j)")
-            )
+        def so():
+            nc.scalar.copy(out=h1_out[:], in_=psum["h1"][:].rearrange("t j p -> t p j"))
+            nc.sync.dma_start(out=out_0[1], in_=h1_out[:].rearrange("t p j -> t (p j)"))
 
-        def hq():
+        def hq(e):
             nc.vector.quantize_mx(
-                out=h_codes[:].bitcast(FP8X4),
-                scales=h_scales[:],
-                in_=h_grouped[:].rearrange("p e t k -> p (e t k)"),
+                out=h_codes[:, e * T : (e + 1) * T].bitcast(FP8X4),
+                scales=h_scales[:, e * T : (e + 1) * T],
+                in_=h_grouped[:, e].rearrange("p t k -> p (t k)"),
             )
 
         a_grouped = keep.tile([P, E, R, PACK], BF16, align_bytes=64)
@@ -321,37 +320,39 @@ def tile_loralinearexpertswrapper_pa_s_kernel(tc, x, low_gu, W_gu, B_gu, A_d, ou
                 in_=a_grouped[:].rearrange("q e r k -> q (e r k)"),
             )
 
-        def lm():
-            psum["low_d"] = flip.tile([P, E, R], F32, tag="flip", name="low_d_ps")
-            for e in range(E):
-                nc.tensor.matmul_mx(
-                    out=psum["low_d"][:, e, :],
-                    lhsT=h_codes[:, e * T : (e + 1) * T].bitcast(FP8X4),
-                    lhsT_scale=h_scales[:, e * T : (e + 1) * T],
-                    rhs=a_codes[:, e * R : (e + 1) * R].bitcast(FP8X4),
-                    rhs_scale=a_scales[:, e * R : (e + 1) * R],
-                    start=True,
-                    stop=True,
-                )
+        def lm(e):
+            if e == 0:
+                psum["low_d"] = flip.tile([P, E, R], F32, tag="flip", name="low_d_ps")
+            nc.tensor.matmul_mx(
+                out=psum["low_d"][:, e, :],
+                lhsT=h_codes[:, e * T : (e + 1) * T].bitcast(FP8X4),
+                lhsT_scale=h_scales[:, e * T : (e + 1) * T],
+                rhs=a_codes[:, e * R : (e + 1) * R].bitcast(FP8X4),
+                rhs_scale=a_scales[:, e * R : (e + 1) * R],
+                start=True,
+                stop=True,
+            )
 
         def lx():
             low_d_sb = keep.tile([P, E, R], F32)
-            nc.scalar.copy(out=low_d_sb[:], in_=psum["low_d"][:])
+            nc.vector.tensor_copy(out=low_d_sb[:], in_=psum["low_d"][:])
             nc.sync.dma_start(out=out_1.rearrange("e t r -> t e r"), in_=low_d_sb[:])
 
         lowt()
         lowx()
-        bt(0)
-        bx(0, "V")
+        bt(0, (GATE,))
+        bx(0, (GATE,), "V")
         xt()
         xx()
+        bt(0, (UP,))
+        bx(0, (UP,), "V")
+        dm(0, GATE)
+        xq()
         wt(0)
         wx(0, "S")
+        dx(0, GATE)
         wt(1)
         wx(1, "V")
-        xq()
-        dm(0, GATE)
-        dx(0, GATE)
         wt(2)
         wx(2, "S")
         wq(0)
@@ -359,8 +360,8 @@ def tile_loralinearexpertswrapper_pa_s_kernel(tc, x, low_gu, W_gu, B_gu, A_d, ou
         wx(3, "V")
         dm(0, UP)
         dx(0, UP)
-        bt(1)
-        bx(1, "S")
+        bt(1, (GATE, UP))
+        bx(1, (GATE, UP), "S")
         wq(1)
         wt(4)
         wx(4, "S")
@@ -378,25 +379,25 @@ def tile_loralinearexpertswrapper_pa_s_kernel(tc, x, low_gu, W_gu, B_gu, A_d, ou
         dm(1, GATE)
         dx(1, GATE)
         silu(0)
+        wq(3)
+        at()
+        mm(2)
         dm(1, UP)
         dx(1, UP)
-        wq(3)
-        mm(2)
-        at()
-        ax()
         mm(3)
         add(1, GATE)
         silu(1)
+        ax()
         pr0()
         ht0()
         hx0()
         add(1, UP)
-        aq()
         pr1()
         ht1()
-        so(0)
-        so(1)
+        so()
+        aq()
         ro1()
-        hq()
-        lm()
+        for e in range(E):
+            hq(e)
+            lm(e)
         lx()

@@ -22,8 +22,8 @@ HALVES = 2
 J = D // P
 JS = 2
 PIECES = J // JS
-WARM_PASSES = 3
-WARM_N = 256
+WARM_PASSES = 12
+WARM_N = 128
 
 FLOPS = 2 * E * T * (H * 2 * D + R * 2 * D + D * R)
 
@@ -59,12 +59,14 @@ def tile_loralinearexpertswrapper_pa_s_kernel(tc, x, low_gu, W_gu, B_gu, A_d, ou
         )
         load_w(0, GATE)
         load_w(0, UP)
-        load_b(1)
         load_w(1, GATE)
+        load_b(1)
         load_w(1, UP)
         a_sb = keep.tile([P, E, D], BF16)
         nc.sync.dma_start(out=a_sb[:], in_=A_d.rearrange("e r d -> r e d"))
 
+        zeros = keep.tile([P, WARM_N * PACK], BF16, align_bytes=64)
+        nc.vector.memset(zeros[:].bitcast(I32), 0)
         ident_bf16 = keep.tile([P, P], BF16)
         ident_f32 = keep.tile([P, P], F32)
         for ident in (ident_bf16, ident_f32):
@@ -75,8 +77,6 @@ def tile_loralinearexpertswrapper_pa_s_kernel(tc, x, low_gu, W_gu, B_gu, A_d, ou
         unused = keep.tile([P, 1], F32)
         nc.scalar.activation(out=unused[:], in_=zero[:], func=ACT.Silu)
 
-        zeros = keep.tile([P, WARM_N * PACK], BF16, align_bytes=64)
-        nc.vector.memset(zeros[:].bitcast(I32), 0)
         zero_codes = keep.tile([P, WARM_N], U32, align_bytes=64)
         zero_scales = keep.tile([P, WARM_N], U8, align_bytes=64)
         nc.vector.quantize_mx(out=zero_codes[:].bitcast(FP8X4), scales=zero_scales[:], in_=zeros[:])
@@ -360,13 +360,13 @@ def tile_loralinearexpertswrapper_pa_s_kernel(tc, x, low_gu, W_gu, B_gu, A_d, ou
         wx(3, "V")
         dm(0, UP)
         dx(0, UP)
-        bt(1, (GATE, UP))
-        bx(1, (GATE, UP), "S")
         wq(1)
         wt(4)
         wx(4, "S")
         wt(5)
         wx(5, "V")
+        bt(1, (GATE, UP))
+        bx(1, (GATE, UP), "S")
         mm(0)
         add(0, GATE)
         wt(6)

from contextlib import ExitStack

import concourse.mybir as mybir
from concourse.masks import make_identity

F32 = mybir.dt.float32
BF16 = mybir.dt.bfloat16
U32 = mybir.dt.uint32
U8 = mybir.dt.uint8
I32 = mybir.dt.int32
FP8X4 = mybir.dt.float8_e4m3fn_x4
ACT = mybir.ActivationFunctionType
ALU = mybir.AluOpType

E, T, H, D, R = 2, 128, 512, 512, 128
LORA_SCALE = 2.0
P = 128
PACK = 4
PAIR = 2
GATE, UP = 0, 1
HALVES = 2
J = D // P
JS = 2
PIECES = J // JS
WARM_PASSES = 12
WARM_N = 128

FLOPS = 2 * E * T * (H * 2 * D + R * 2 * D + D * R)


def tile_loralinearexpertswrapper_pa_s_kernel(tc, x, low_gu, W_gu, B_gu, A_d, out_0, out_1):
    nc = tc.nc
    with ExitStack() as ctx:
        keep = ctx.enter_context(tc.tile_pool(name="keep", bufs=1))
        work = ctx.enter_context(tc.tile_pool(name="work", bufs=4))
        flip = ctx.enter_context(tc.psum_pool(name="flip", bufs=4))
        sums = ctx.enter_context(tc.psum_pool(name="sums", bufs=4))
        ctx.enter_context(tc.manual_schedule())

        low_sb = keep.tile([P, E, R], BF16)
        nc.sync.dma_start(out=low_sb[:], in_=low_gu.rearrange("e t r -> t e r"))
        b_sb = {}
        w_sb = {}

        def load_b(e):
            b_sb[e] = keep.tile([P, HALVES, J * R], BF16, name="b_sb_%d" % e)
            nc.sync.dma_start(out=b_sb[e][:], in_=B_gu.rearrange("e (s p j) r -> e p s (j r)", s=HALVES, p=P)[e])

        def load_w(e, s):
            w_sb[(e, s)] = keep.tile([P, J, H], BF16, name="w_sb_%d_%d" % (e, s))
            nc.sync.dma_start(
                out=w_sb[(e, s)][:], in_=W_gu.rearrange("e (s p j) h -> e s p j h", s=HALVES, p=P)[e, s]
            )

        load_b(0)
        x_sb = keep.tile([P, PAIR, H], BF16)
        nc.sync.dma_start(
            out=x_sb[:], in_=x.rearrange("e t h -> (e t) h").rearrange("(p i) h -> p i h", i=PAIR)
        )
        load_w(0, GATE)
        load_w(0, UP)
        load_w(1, GATE)
        load_b(1)
        load_w(1, UP)
        a_sb = keep.tile([P, E, D], BF16)
        nc.sync.dma_start(out=a_sb[:], in_=A_d.rearrange("e r d -> r e d"))

        zeros = keep.tile([P, WARM_N * PACK], BF16, align_bytes=64)
        nc.vector.memset(zeros[:].bitcast(I32), 0)
        ident_bf16 = keep.tile([P, P], BF16)
        ident_f32 = keep.tile([P, P], F32)
        for ident in (ident_bf16, ident_f32):
            nc.vector.memset(ident[:], 0.0)
            make_identity(nc, ident[:], nomemset=True)
        zero = keep.tile([P, 1], F32)
        nc.vector.memset(zero[:], 0.0)
        unused = keep.tile([P, 1], F32)
        nc.scalar.activation(out=unused[:], in_=zero[:], func=ACT.Silu)

        zero_codes = keep.tile([P, WARM_N], U32, align_bytes=64)
        zero_scales = keep.tile([P, WARM_N], U8, align_bytes=64)
        nc.vector.quantize_mx(out=zero_codes[:].bitcast(FP8X4), scales=zero_scales[:], in_=zeros[:])
        warm_ps = sums.tile([P, WARM_N], F32, tag="sums")
        for i in range(WARM_PASSES):
            nc.tensor.matmul_mx(
                out=warm_ps[:],
                lhsT=zero_codes[:, :P].bitcast(FP8X4),
                lhsT_scale=zero_scales[:, :P],
                rhs=zero_codes[:].bitcast(FP8X4),
                rhs_scale=zero_scales[:],
                start=True,
                stop=True,
            )

        def copy_out(engine, out, in_):
            if engine == "S":
                nc.scalar.copy(out=out, in_=in_)
            else:
                nc.vector.tensor_copy(out=out, in_=in_)

        psum = {}

        def from_psum(e, ap):
            return ap.rearrange("t (j p) -> t p j", j=J) if e == 0 else ap

        def by_d(e, ap):
            return ap.rearrange("t (p j) -> t p j", j=J) if e == 0 else ap

        low_k = keep.tile([P, E, T], BF16)
        b_k = keep.tile([P, E, HALVES, J, P], BF16)
        delta = keep.tile([P, E, HALVES, J * P], F32)

        def lowt():
            psum["low"] = flip.tile([P, E, T], BF16, tag="flip", name="low_t")
            for e in range(E):
                nc.tensor.transpose(psum["low"][:, e, :], low_sb[:, e, :], ident_bf16[:])

        def lowx():
            nc.scalar.copy(out=low_k[:], in_=psum["low"][:])

        def bt(e, ss):
            psum[("b", e, ss[0])] = flip.tile([P, len(ss), J, P], BF16, tag="flip", name="b_t")
            for s in ss:
                for j in range(J):
                    nc.tensor.transpose(
                        psum[("b", e, ss[0])][:, s - ss[0], j, :], b_sb[e][:, s, j * R : (j + 1) * R], ident_bf16[:]
                    )

        def bx(e, ss, engine):
            copy_out(engine, b_k[:, e, ss[0] : ss[-1] + 1], psum[("b", e, ss[0])][:])

        def dm(e, s):
            psum[("d", e, s)] = sums.tile([P, J * P], F32, tag="sums", name="delta_ps")
            if e == 0:
                nc.tensor.matmul(
                    psum[("d", e, s)][:],
                    lhsT=low_k[:, e, :],
                    rhs=b_k[:, e, s].rearrange("r j p -> r (j p)"),
                    start=True,
                    stop=True,
                )
            else:
                for j in range(J):
                    nc.tensor.matmul(
                        psum[("d", e, s)][:, j * T : (j + 1) * T],
                        lhsT=b_k[:, e, s, j, :],
                        rhs=low_k[:, e, :],
                        start=True,
                        stop=True,
                    )

        def dx(e, s):
            nc.scalar.copy(out=by_d(e, delta[:, e, s]), in_=from_psum(e, psum[("d", e, s)][:]))

        def xt():
            words = x_sb[:].bitcast(F32)
            psum["x"] = flip.tile([P, PAIR, PAIR, P], F32, tag="flip", name="x_t")
            for i in range(PAIR):
                for u in range(PAIR):
                    nc.tensor.transpose(psum["x"][:, i, u, :], words[:, i, u * P : (u + 1) * P], ident_f32[:])

        x_grouped = keep.tile([P, P, PAIR, PACK], BF16, align_bytes=64)
        x_codes = keep.tile([P, E * T], U32, align_bytes=64)
        x_scales = keep.tile([P, E * T], U8, align_bytes=64)

        def xx():
            nc.vector.tensor_copy(out=x_grouped[:].bitcast(F32), in_=psum["x"][:].rearrange("q i u p -> q p i u"))

        def xq():
            nc.vector.quantize_mx(
                out=x_codes[:].bitcast(FP8X4),
                scales=x_scales[:],
                in_=x_grouped[:].rearrange("q p i k -> q (p i k)"),
            )

        halves = [(e, s) for e in range(E) for s in range(HALVES)]
        w_grouped = {}
        w_codes = {}
        w_scales = {}

        def wt(m):
            words = w_sb[halves[m // PIECES]][:].bitcast(F32)
            psum[("w", m)] = flip.tile([P, JS, PAIR, P], F32, tag="flip", name="w_t")
            for j in range(JS):
                for u in range(PAIR):
                    nc.tensor.transpose(
                        psum[("w", m)][:, j, u, :],
                        words[:, m % PIECES * JS + j, u * P : (u + 1) * P],
                        ident_f32[:],
                    )

        def wx(m, engine):
            n, c = m // PIECES, m % PIECES
            if n not in w_grouped:
                w_grouped[n] = work.tile([P, J, P, PACK], BF16, align_bytes=64, name="w_grouped")
            copy_out(
                engine,
                w_grouped[n][:, c * JS : (c + 1) * JS].bitcast(F32),
                psum[("w", m)][:].rearrange("q j u p -> q j p u"),
            )

        def wq(n):
            w_codes[n] = work.tile([P, J * P], U32, align_bytes=64, name="w_codes")
            w_scales[n] = work.tile([P, J * P], U8, align_bytes=64, name="w_scales")
            nc.vector.quantize_mx(
                out=w_codes[n][:].bitcast(FP8X4),
                scales=w_scales[n][:],
                in_=w_grouped[n][:].rearrange("q j p k -> q (j p k)"),
            )

        def mm(n):
            e, s = halves[n]
            psum[("base", e, s)] = sums.tile([P, J * P], F32, tag="sums", name="base")
            out = psum[("base", e, s)]
            x_c, x_s = x_codes[:, e * T : (e + 1) * T].bitcast(FP8X4), x_scales[:, e * T : (e + 1) * T]
            if e == 0:
                nc.tensor.matmul_mx(
                    out=out[:],
                    lhsT=x_c,
                    lhsT_scale=x_s,
                    rhs=w_codes[n][:].bitcast(FP8X4),
                    rhs_scale=w_scales[n][:],
                    start=True,
                    stop=True,
                )
            else:
                for j in range(J):
                    one = slice(j * P, (j + 1) * P)
                    nc.tensor.matmul_mx(
                        out=out[:, one],
                        lhsT=w_codes[n][:, one].bitcast(FP8X4),
                        lhsT_scale=w_scales[n][:, one],
                        rhs=x_c,
                        rhs_scale=x_s,
                        start=True,
                        stop=True,
                    )

        total = {(e, s): keep.tile([P, J * P], F32, name="total_%d_%d" % (e, s)) for e in range(E) for s in range(HALVES)}
        gate_act = {e: keep.tile([P, J * P], F32, name="gate_act_%d" % e) for e in range(E)}
        def add(e, s):
            nc.vector.scalar_tensor_tensor(
                out=by_d(e, total[(e, s)][:]),
                in0=by_d(e, delta[:, e, s]),
                scalar=LORA_SCALE,
                in1=from_psum(e, psum[("base", e, s)][:]),
                op0=ALU.mult,
                op1=ALU.add,
            )

        def silu(e):
            nc.scalar.activation(out=gate_act[e][:], in_=total[(e, GATE)][:], func=ACT.Silu)

        h_grouped = keep.tile([P, E, T, PACK], BF16, align_bytes=64)
        h_codes = keep.tile([P, E * T], U32, align_bytes=64)
        h_scales = keep.tile([P, E * T], U8, align_bytes=64)
        h0 = keep.tile([P, D], F32)
        h1 = keep.tile([P, J * P], F32)
        h1_out = keep.tile([P, P, J], F32)

        def pr0():
            nc.vector.tensor_tensor(out=h0[:], in0=total[(0, UP)][:], in1=gate_act[0][:], op=ALU.mult)
            nc.sync.dma_start(out=out_0[0], in_=h0[:])

        def ht0():
            psum["h0"] = flip.tile([P, PAIR, PAIR, T], F32, tag="flip", name="h0_t")
            for u in range(PAIR):
                for i in range(PAIR):
                    nc.tensor.transpose(
                        psum["h0"][:, u, i, :], h0[:, u * PAIR * P + i : (u + 1) * PAIR * P : PAIR], ident_f32[:]
                    )

        def hx0():
            nc.scalar.copy(
                out=h_grouped[:, 0].rearrange("q t (u i) -> q t u i", u=PAIR),
                in_=psum["h0"][:].rearrange("q u i t -> q t u i"),
            )

        def pr1():
            nc.vector.tensor_tensor(out=h1[:], in0=total[(1, UP)][:], in1=gate_act[1][:], op=ALU.mult)

        def ro1():
            nc.vector.tensor_copy(out=h_grouped[:, 1], in_=h1[:].rearrange("p (j t) -> p t j", j=J))

        def ht1():
            psum["h1"] = flip.tile([P, J, P], F32, tag="flip", name="h1_t")
            for j in range(J):
                nc.tensor.transpose(psum["h1"][:, j, :], h1[:, j * T : (j + 1) * T], ident_f32[:])

        def so():
            nc.scalar.copy(out=h1_out[:], in_=psum["h1"][:].rearrange("t j p -> t p j"))
            nc.sync.dma_start(out=out_0[1], in_=h1_out[:].rearrange("t p j -> t (p j)"))

        def hq(e):
            nc.vector.quantize_mx(
                out=h_codes[:, e * T : (e + 1) * T].bitcast(FP8X4),
                scales=h_scales[:, e * T : (e + 1) * T],
                in_=h_grouped[:, e].rearrange("p t k -> p (t k)"),
            )

        a_grouped = keep.tile([P, E, R, PACK], BF16, align_bytes=64)
        a_codes = keep.tile([P, E * R], U32, align_bytes=64)
        a_scales = keep.tile([P, E * R], U8, align_bytes=64)

        def at():
            words = a_sb[:].bitcast(F32)
            psum["a"] = flip.tile([P, E, PAIR, R], F32, tag="flip", name="a_t")
            for u in range(PAIR):
                nc.tensor.transpose(psum["a"][:, 0, u, :], words[:, 0, u * P : (u + 1) * P], ident_f32[:])
            for u in range(PAIR):
                nc.tensor.transpose(psum["a"][:, 1, u, :], words[:, 1, u::PAIR], ident_f32[:])

        def ax():
            nc.scalar.copy(out=a_grouped[:].bitcast(F32), in_=psum["a"][:].rearrange("q e u r -> q e r u"))

        def aq():
            nc.vector.quantize_mx(
                out=a_codes[:].bitcast(FP8X4),
                scales=a_scales[:],
                in_=a_grouped[:].rearrange("q e r k -> q (e r k)"),
            )

        def lm(e):
            if e == 0:
                psum["low_d"] = flip.tile([P, E, R], F32, tag="flip", name="low_d_ps")
            nc.tensor.matmul_mx(
                out=psum["low_d"][:, e, :],
                lhsT=h_codes[:, e * T : (e + 1) * T].bitcast(FP8X4),
                lhsT_scale=h_scales[:, e * T : (e + 1) * T],
                rhs=a_codes[:, e * R : (e + 1) * R].bitcast(FP8X4),
                rhs_scale=a_scales[:, e * R : (e + 1) * R],
                start=True,
                stop=True,
            )

        def lx():
            low_d_sb = keep.tile([P, E, R], F32)
            nc.vector.tensor_copy(out=low_d_sb[:], in_=psum["low_d"][:])
            nc.sync.dma_start(out=out_1.rearrange("e t r -> t e r"), in_=low_d_sb[:])

        lowt()
        lowx()
        bt(0, (GATE,))
        bx(0, (GATE,), "V")
        xt()
        xx()
        bt(0, (UP,))
        bx(0, (UP,), "V")
        dm(0, GATE)
        xq()
        wt(0)
        wx(0, "S")
        dx(0, GATE)
        wt(1)
        wx(1, "V")
        wt(2)
        wx(2, "S")
        wq(0)
        wt(3)
        wx(3, "V")
        dm(0, UP)
        dx(0, UP)
        wq(1)
        wt(4)
        wx(4, "S")
        wt(5)
        wx(5, "V")
        bt(1, (GATE, UP))
        bx(1, (GATE, UP), "S")
        mm(0)
        add(0, GATE)
        wt(6)
        wx(6, "S")
        wq(2)
        wt(7)
        wx(7, "S")
        mm(1)
        add(0, UP)
        dm(1, GATE)
        dx(1, GATE)
        silu(0)
        wq(3)
        at()
        mm(2)
        dm(1, UP)
        dx(1, UP)
        mm(3)
        add(1, GATE)
        silu(1)
        ax()
        pr0()
        ht0()
        hx0()
        add(1, UP)
        pr1()
        ht1()
        so()
        aq()
        ro1()
        for e in range(E):
            hq(e)
            lm(e)
        lx()
